import numpy as np
import ml_dtypes


def mxq(x, axis, fmt="e4m3"):
    dtype, down = {"e4m3": (ml_dtypes.float8_e4m3fn, 7), "e5m2": (ml_dtypes.float8_e5m2, 14)}[fmt]
    v = np.moveaxis(np.asarray(x, np.float32).astype(ml_dtypes.bfloat16).astype(np.float64), axis, -1)
    blocks = v.reshape(v.shape[:-1] + (-1, 32))
    amax = np.abs(blocks).max(-1, keepdims=True)
    byte = np.maximum(np.where(amax > 0, np.frexp(amax)[1] - 1 + 127, 0) - down, 1)
    scale = np.exp2(byte - 127.0)
    codes = (blocks / scale).astype(np.float32).astype(dtype).astype(np.float64)
    return np.moveaxis((codes * scale).reshape(v.shape), -1, axis)


WIDE = False


def mx_kscale(k):
    if not WIDE:
        return np.ones(k)
    levels = np.array([10, -10, 5, -5, 0])
    a = np.random.permutation(np.resize(levels, k // 512 * 4)).reshape(k // 512, 4)
    idx = np.arange(k)
    return np.exp2(a[idx // 512, idx % 128 // 32])


BF16 = ml_dtypes.bfloat16


def bf(x):
    return np.asarray(x, np.float32).astype(BF16)


def f64(x):
    return np.asarray(x).astype(np.float64)


B, S, N, D = 32, 256, 512, 1024


def setup_inputs():
    s = mx_kscale(N)
    return {"input_numeric": bf(np.random.standard_normal((B, S, 1))),
            "proj_w": bf(np.random.standard_normal((N, 1))),
            "proj_b": bf(np.random.standard_normal(N) + np.log(s)),
            "emb_table": bf(np.random.standard_normal((N, D)) * 0.15 * np.sqrt(N) * np.mean(s) / s[:, None])}


def reference(input_numeric, proj_w, proj_b, emb_table):
    logits = f64(input_numeric) * f64(proj_w)[:, 0] + f64(proj_b)
    e = np.exp(logits - logits.max(-1, keepdims=True))
    weights = e / e.sum(-1, keepdims=True)
    return mxq(weights, 2, "e4m3") @ mxq(f64(emb_table), 0, "e4m3")

@@ -1,0 +1,256 @@
+from contextlib import ExitStack
+
+import concourse.mybir as mybir
+from concourse.masks import make_identity
+
+F32 = mybir.dt.float32
+BF16 = mybir.dt.bfloat16
+U32 = mybir.dt.uint32
+U8 = mybir.dt.uint8
+FP8X4 = mybir.dt.float8_e4m3fn_x4
+ALU = mybir.AluOpType
+ACT = mybir.ActivationFunctionType
+AX = mybir.AxisListType
+
+P = 128
+PACK = 4
+T = 32 * 256
+N = 512
+D = 1024
+HALF = 512
+PAIR = 2
+PAIRS = T // (P * PAIR)
+MM_CHUNKS = 3
+BLOCK = 1024
+ONES_ROW = 32
+BLOCKS = ((0, 256), (256, 768)) + tuple([(i * BLOCK, BLOCK) for i in range(1, T // BLOCK)])
+TWO_ONES = 1.0019378662109375
+FILL = 2
+TAIL = 3
+VECTOR_SHARE = ((0, 0),)
+
+FLOPS = 2 * T * N * D
+
+
+def tile_softembedding_t_kernel(tc, input_numeric, proj_w, proj_b, emb_table, out):
+    nc = tc.nc
+    x_row = input_numeric.rearrange("b s o -> o (b s)")
+    x_flat = input_numeric.rearrange("b s o -> (b s o)")
+    out_rows = out.rearrange("b s d -> (b s) d")
+
+    with ExitStack() as ctx:
+        keep = ctx.enter_context(tc.tile_pool(name="keep", bufs=1))
+        logit_pool = ctx.enter_context(tc.tile_pool(name="logit", bufs=3))
+        work = ctx.enter_context(tc.tile_pool(name="work", bufs=6))
+        small = ctx.enter_context(tc.tile_pool(name="small", bufs=6))
+        quant = ctx.enter_context(tc.tile_pool(name="quant", bufs=3))
+        store = ctx.enter_context(tc.tile_pool(name="store", bufs=6))
+        ps_logit = ctx.enter_context(tc.psum_pool(name="ps_logit", bufs=2))
+        ps_flip = ctx.enter_context(tc.psum_pool(name="ps_flip", bufs=2))
+        ps_out = ctx.enter_context(tc.psum_pool(name="ps_out", bufs=4))
+
+        wb_raw = keep.tile([P, N], BF16)
+        x_rows = keep.tile([P, T], BF16)
+        x_all = keep.tile([P, T], BF16)
+        w4_raw = keep.tile([P, PACK], BF16)
+        b4_raw = keep.tile([P, PACK], BF16)
+        emb_raw = keep.tile([P, PACK, D], BF16)
+        ident_f32 = keep.tile([P, P], F32)
+        ident_bf16 = keep.tile([P, P], BF16)
+        wb_neg = keep.tile([P, PACK, P], BF16)
+        neg_w4 = keep.tile([P, PACK], F32)
+        neg_b4 = keep.tile([P, PACK], F32)
+        emb_grouped = keep.tile([P, D, PACK], BF16, align_bytes=64)
+        emb_codes = keep.tile([P, D], U32, align_bytes=64)
+        emb_scales = keep.tile([P, D], U8, align_bytes=64)
+
+        def load_and_prepare():
+            first = BLOCKS[1][0]
+            second = BLOCKS[2][0]
+            nc.vector.memset(wb_raw[:], 0.0)
+            nc.vector.memset(x_rows[:, 0:second], 1.0)
+            nc.scalar.dma_start(out=w4_raw[:], in_=proj_w.rearrange("(i c) o -> i (c o)", c=PACK))
+            nc.scalar.dma_start(out=b4_raw[:], in_=proj_b.rearrange("(i c) -> i c", c=PACK))
+            nc.scalar.dma_start(out=x_all[:, 0:first], in_=x_flat[0:first].partition_broadcast(P))
+            nc.sync.dma_start(out=wb_raw[0:1, :], in_=proj_w.rearrange("n o -> o n"))
+            nc.sync.dma_start(out=wb_raw[ONES_ROW : ONES_ROW + 1, :], in_=proj_b.rearrange("(o n) -> o n", o=1))
+            nc.sync.dma_start(out=x_rows[0:1, 0:second], in_=x_row[:, 0:second])
+            nc.scalar.dma_start(out=x_all[:, first:second], in_=x_flat[first:second].partition_broadcast(P))
+            nc.sync.dma_start(out=emb_raw[:], in_=emb_table.rearrange("(p j) d -> p j d", j=PACK))
+            nc.scalar.dma_start(out=x_all[:, second:T], in_=x_flat[second:T].partition_broadcast(P))
+            make_identity(nc, ident_f32[:])
+            nc.vector.tensor_scalar(out=neg_w4[:], in0=w4_raw[:], scalar1=-1.0, scalar2=None, op0=ALU.mult)
+            nc.vector.tensor_scalar(out=neg_b4[:], in0=b4_raw[:], scalar1=-1.0, scalar2=None, op0=ALU.mult)
+            nc.vector.tensor_scalar(
+                out=wb_neg[:], in0=wb_raw[:].rearrange("p (i c) -> p c i", c=PACK), scalar1=-1.0, scalar2=None,
+                op0=ALU.mult,
+            )
+            gpsimd_logits(0)
+            make_identity(nc, ident_bf16[:])
+            nc.gpsimd.memset(x_rows[:, second:T].bitcast(F32), TWO_ONES)
+            nc.sync.dma_start(out=x_rows[0:1, second:T], in_=x_row[:, second:T])
+            gpsimd_logits(1)
+
+        def regroup_table(half):
+            cols = slice(half * HALF, (half + 1) * HALF)
+            nc.scalar.copy(out=emb_grouped[:, cols, :], in_=emb_raw[:, :, cols].rearrange("p j d -> p d j"))
+
+        def quantise_table():
+            nc.vector.quantize_mx(
+                out=emb_codes[:].bitcast(FP8X4),
+                scales=emb_scales[:],
+                in_=emb_grouped[:].rearrange("p d j -> p (d j)"),
+            )
+
+        last_chunk = {}
+        banks = {}
+        exps = {}
+        inverses = {}
+        weights = {}
+        flips = {}
+        packed = {}
+
+        def gpsimd_logits(block):
+            start, size = BLOCKS[block]
+            tile = logit_pool.tile([P, BLOCK], F32, name="neg_last")
+            nc.gpsimd.tensor_scalar(
+                out=tile[:, 0:size],
+                in0=x_all[:, start : start + size],
+                scalar1=neg_w4[:, MM_CHUNKS : MM_CHUNKS + 1],
+                scalar2=neg_b4[:, MM_CHUNKS : MM_CHUNKS + 1],
+                op0=ALU.mult,
+                op1=ALU.add,
+            )
+            last_chunk[block] = tile
+
+        def logits(k):
+            for u in range(PAIR):
+                t0 = (k * PAIR + u) * P
+                bank = ps_logit.tile([P, N], F32, name="bank")
+                nc.tensor.matmul(
+                    out=bank[:, 0 : MM_CHUNKS * P],
+                    lhsT=x_rows[:, t0 : t0 + P],
+                    rhs=wb_neg[:, 0:MM_CHUNKS, :].rearrange("p c i -> p (c i)"),
+                    start=True,
+                    stop=True,
+                )
+                block = max([i for i in range(len(BLOCKS)) if BLOCKS[i][0] <= t0])
+                at = t0 - BLOCKS[block][0]
+                nc.tensor.transpose(bank[:, MM_CHUNKS * P : N], last_chunk[block][:, at : at + P], ident_f32[:])
+                banks[(k, u)] = bank
+
+        totals = {}
+
+        def maxima_and_exps(k):
+            neg_max = small.tile([P, PAIR], F32, name="neg_max")
+            total = small.tile([P, PAIR], F32, name="total")
+            for u in range(PAIR):
+                bank = banks[(k, u)]
+                nc.vector.tensor_reduce(out=neg_max[:, u : u + 1], in_=bank[:], axis=AX.X, op=ALU.min)
+                e = work.tile([P, N], F32, name="exps")
+                nc.scalar.activation(
+                    out=e[:], in_=bank[:], func=ACT.Exp, bias=neg_max[:, u : u + 1], scale=-1.0,
+                    accum_out=total[:, u : u + 1],
+                )
+                exps[(k, u)] = e
+            totals[k] = total
+
+        def reciprocals(k):
+            inverse = small.tile([P, PAIR], F32, name="inverse")
+            nc.vector.reciprocal(out=inverse[:], in_=totals[k][:])
+            inverses[k] = inverse
+
+        def normalise(k):
+            for u in range(PAIR):
+                w = work.tile([P, N], BF16, name="weights")
+                nc.gpsimd.tensor_scalar(
+                    out=w[:], in0=exps[(k, u)][:], scalar1=inverses[k][:, u : u + 1], scalar2=0.0,
+                    op0=ALU.mult, op1=ALU.add,
+                )
+                weights[(k, u)] = w
+
+        def flip(k):
+            flipped = ps_flip.tile([P, PAIR, PACK, P], BF16, name="flipped")
+            for u in range(PAIR):
+                for c in range(PACK):
+                    nc.tensor.transpose(flipped[:, u, c, :], weights[(k, u)][:, c * P : (c + 1) * P], ident_bf16[:])
+            flips[k] = flipped
+
+        groupeds = {}
+
+        def group(k):
+            grouped = quant.tile([P, PAIR, P, PACK], BF16, name="grouped", align_bytes=64)
+            if k < FILL:
+                nc.scalar.copy(out=grouped[:], in_=flips[k][:].rearrange("p u c t -> p u t c"))
+            else:
+                nc.vector.tensor_copy(out=grouped[:], in_=flips[k][:].rearrange("p u c t -> p u t c"))
+            groupeds[k] = grouped
+
+        def quantise(k):
+            codes = quant.tile([P, PAIR * P], U32, name="codes", align_bytes=64)
+            scales = quant.tile([P, PAIR * P], U8, name="scales", align_bytes=64)
+            nc.vector.quantize_mx(
+                out=codes[:].bitcast(FP8X4), scales=scales[:], in_=groupeds[k][:].rearrange("p u t c -> p (u t c)")
+            )
+            packed[k] = (codes, scales)
+
+        accs = {}
+
+        def passes(k):
+            codes, scales = packed[k]
+            for u in range(PAIR):
+                for h in range(D // HALF):
+                    acc = ps_out.tile([P, HALF], F32, name="acc")
+                    nc.tensor.matmul_mx(
+                        out=acc[:],
+                        lhsT=codes[:, u * P : (u + 1) * P].bitcast(FP8X4),
+                        lhsT_scale=scales[:, u * P : (u + 1) * P],
+                        rhs=emb_codes[:, h * HALF : (h + 1) * HALF].bitcast(FP8X4),
+                        rhs_scale=emb_scales[:, h * HALF : (h + 1) * HALF],
+                        start=True,
+                        stop=True,
+                    )
+                    accs[(k, u, h)] = acc
+
+        def drain(k):
+            for u in range(PAIR):
+                t0 = (k * PAIR + u) * P
+                result = store.tile([P, D], F32, name="result")
+                for h in range(D // HALF):
+                    if (u, h) in VECTOR_SHARE or (k >= PAIRS - TAIL and h == 0):
+                        nc.vector.tensor_copy(out=result[:, h * HALF : (h + 1) * HALF], in_=accs[(k, u, h)][:])
+                    else:
+                        nc.scalar.copy(out=result[:, h * HALF : (h + 1) * HALF], in_=accs[(k, u, h)][:])
+                nc.sync.dma_start(out=out_rows[t0 : t0 + P, :], in_=result[:])
+
+        def live(k):
+            return 0 <= k < PAIRS
+
+        with tc.manual_schedule():
+            load_and_prepare()
+            logits(0)
+            for s in range(PAIRS + 4):
+                if live(s):
+                    maxima_and_exps(s)
+                if s < 2:
+                    regroup_table(s)
+                if live(s - 1):
+                    flip(s - 1)
+                if live(s - 3):
+                    drain(s - 3)
+                if s == 2:
+                    quantise_table()
+                if live(s - 2):
+                    quantise(s - 2)
+                if live(s):
+                    reciprocals(s)
+                if live(s - 1):
+                    group(s - 1)
+                if live(s):
+                    normalise(s)
+                    if s % 4 == 1 and (s + 7) // 4 < len(BLOCKS):
+                        gpsimd_logits((s + 7) // 4)
+                if live(s + 1):
+                    logits(s + 1)
+                if live(s - 2):
+                    passes(s - 2)

@@ -22,11 +22,9 @@ PAIR = 2
 PAIRS = T // (P * PAIR)
 MM_CHUNKS = 3
 BLOCK = 1024
+BLOCK_PAIRS = BLOCK // (P * PAIR)
 ONES_ROW = 32
-BLOCKS = ((0, 256), (256, 768)) + tuple([(i * BLOCK, BLOCK) for i in range(1, T // BLOCK)])
 TWO_ONES = 1.0019378662109375
-FILL = 2
-TAIL = 3
 VECTOR_SHARE = ((0, 0),)
 
 FLOPS = 2 * T * N * D
@@ -40,7 +38,7 @@ def tile_softembedding_t_kernel(tc, input_numeric, proj_w, proj_b, emb_table, ou
 
     with ExitStack() as ctx:
         keep = ctx.enter_context(tc.tile_pool(name="keep", bufs=1))
-        logit_pool = ctx.enter_context(tc.tile_pool(name="logit", bufs=3))
+        logit_pool = ctx.enter_context(tc.tile_pool(name="logit", bufs=2))
         work = ctx.enter_context(tc.tile_pool(name="work", bufs=6))
         small = ctx.enter_context(tc.tile_pool(name="small", bufs=6))
         quant = ctx.enter_context(tc.tile_pool(name="quant", bufs=3))
@@ -64,32 +62,38 @@ def tile_softembedding_t_kernel(tc, input_numeric, proj_w, proj_b, emb_table, ou
         emb_codes = keep.tile([P, D], U32, align_bytes=64)
         emb_scales = keep.tile([P, D], U8, align_bytes=64)
 
+        last_chunk = {}
+        banks = {}
+        exps = {}
+        totals = {}
+        neg_maxima = {}
+        inverses = {}
+        weights = {}
+        flips = {}
+        groupeds = {}
+        packed = {}
+        accs = {}
+
         def load_and_prepare():
-            first = BLOCKS[1][0]
-            second = BLOCKS[2][0]
-            nc.vector.memset(wb_raw[:], 0.0)
-            nc.vector.memset(x_rows[:, 0:second], 1.0)
-            nc.scalar.dma_start(out=w4_raw[:], in_=proj_w.rearrange("(i c) o -> i (c o)", c=PACK))
-            nc.scalar.dma_start(out=b4_raw[:], in_=proj_b.rearrange("(i c) -> i c", c=PACK))
-            nc.scalar.dma_start(out=x_all[:, 0:first], in_=x_flat[0:first].partition_broadcast(P))
+            nc.vector.memset(wb_raw[:].bitcast(F32), 0.0)
+            nc.vector.memset(x_rows[:, 0:BLOCK].bitcast(F32), TWO_ONES)
             nc.sync.dma_start(out=wb_raw[0:1, :], in_=proj_w.rearrange("n o -> o n"))
             nc.sync.dma_start(out=wb_raw[ONES_ROW : ONES_ROW + 1, :], in_=proj_b.rearrange("(o n) -> o n", o=1))
-            nc.sync.dma_start(out=x_rows[0:1, 0:second], in_=x_row[:, 0:second])
-            nc.scalar.dma_start(out=x_all[:, first:second], in_=x_flat[first:second].partition_broadcast(P))
+            nc.sync.dma_start(out=x_rows[0:1, 0:BLOCK], in_=x_row[:, 0:BLOCK])
+            nc.scalar.dma_start(out=w4_raw[:], in_=proj_w.rearrange("(i c) o -> i (c o)", c=PACK))
+            nc.scalar.dma_start(out=b4_raw[:], in_=proj_b.rearrange("(i c) -> i c", c=PACK))
+            nc.gpsimd.memset(x_rows[:, BLOCK:T].bitcast(F32), TWO_ONES)
             nc.sync.dma_start(out=emb_raw[:], in_=emb_table.rearrange("(p j) d -> p j d", j=PACK))
-            nc.scalar.dma_start(out=x_all[:, second:T], in_=x_flat[second:T].partition_broadcast(P))
+            nc.sync.dma_start(out=x_rows[0:1, BLOCK:T], in_=x_row[:, BLOCK:T])
+            nc.scalar.dma_start(out=x_all[:, BLOCK:T], in_=x_flat[BLOCK:T].partition_broadcast(P))
+            make_identity(nc, ident_bf16[:])
             make_identity(nc, ident_f32[:])
-            nc.vector.tensor_scalar(out=neg_w4[:], in0=w4_raw[:], scalar1=-1.0, scalar2=None, op0=ALU.mult)
-            nc.vector.tensor_scalar(out=neg_b4[:], in0=b4_raw[:], scalar1=-1.0, scalar2=None, op0=ALU.mult)
             nc.vector.tensor_scalar(
                 out=wb_neg[:], in0=wb_raw[:].rearrange("p (i c) -> p c i", c=PACK), scalar1=-1.0, scalar2=None,
                 op0=ALU.mult,
             )
-            gpsimd_logits(0)
-            make_identity(nc, ident_bf16[:])
-            nc.gpsimd.memset(x_rows[:, second:T].bitcast(F32), TWO_ONES)
-            nc.sync.dma_start(out=x_rows[0:1, second:T], in_=x_row[:, second:T])
-            gpsimd_logits(1)
+            nc.vector.tensor_scalar(out=neg_w4[:], in0=w4_raw[:], scalar1=-1.0, scalar2=None, op0=ALU.mult)
+            nc.vector.tensor_scalar(out=neg_b4[:], in0=b4_raw[:], scalar1=-1.0, scalar2=None, op0=ALU.mult)
 
         def regroup_table(half):
             cols = slice(half * HALF, (half + 1) * HALF)
@@ -102,20 +106,11 @@ def tile_softembedding_t_kernel(tc, input_numeric, proj_w, proj_b, emb_table, ou
                 in_=emb_grouped[:].rearrange("p d j -> p (d j)"),
             )
 
-        last_chunk = {}
-        banks = {}
-        exps = {}
-        inverses = {}
-        weights = {}
-        flips = {}
-        packed = {}
-
         def gpsimd_logits(block):
-            start, size = BLOCKS[block]
             tile = logit_pool.tile([P, BLOCK], F32, name="neg_last")
             nc.gpsimd.tensor_scalar(
-                out=tile[:, 0:size],
-                in0=x_all[:, start : start + size],
+                out=tile[:],
+                in0=x_all[:, block * BLOCK : (block + 1) * BLOCK],
                 scalar1=neg_w4[:, MM_CHUNKS : MM_CHUNKS + 1],
                 scalar2=neg_b4[:, MM_CHUNKS : MM_CHUNKS + 1],
                 op0=ALU.mult,
@@ -123,37 +118,34 @@ def tile_softembedding_t_kernel(tc, input_numeric, proj_w, proj_b, emb_table, ou
             )
             last_chunk[block] = tile
 
-        def logits(k):
-            for u in range(PAIR):
-                t0 = (k * PAIR + u) * P
-                bank = ps_logit.tile([P, N], F32, name="bank")
-                nc.tensor.matmul(
-                    out=bank[:, 0 : MM_CHUNKS * P],
-                    lhsT=x_rows[:, t0 : t0 + P],
-                    rhs=wb_neg[:, 0:MM_CHUNKS, :].rearrange("p c i -> p (c i)"),
-                    start=True,
-                    stop=True,
-                )
-                block = max([i for i in range(len(BLOCKS)) if BLOCKS[i][0] <= t0])
-                at = t0 - BLOCKS[block][0]
-                nc.tensor.transpose(bank[:, MM_CHUNKS * P : N], last_chunk[block][:, at : at + P], ident_f32[:])
-                banks[(k, u)] = bank
+        def logits(k, u):
+            t0 = (k * PAIR + u) * P
+            chunks = PACK if t0 < BLOCK else MM_CHUNKS
+            bank = ps_logit.tile([P, N], F32, name="bank")
+            nc.tensor.matmul(
+                out=bank[:, 0 : chunks * P],
+                lhsT=x_rows[:, t0 : t0 + P],
+                rhs=wb_neg[:, 0:chunks, :].rearrange("p c i -> p (c i)"),
+                start=True,
+                stop=True,
+            )
+            if chunks < PACK:
+                at = t0 % BLOCK
+                nc.tensor.transpose(bank[:, MM_CHUNKS * P : N], last_chunk[t0 // BLOCK][:, at : at + P], ident_f32[:])
+            banks[(k, u)] = bank
 
-        totals = {}
-
-        def maxima_and_exps(k):
-            neg_max = small.tile([P, PAIR], F32, name="neg_max")
-            total = small.tile([P, PAIR], F32, name="total")
-            for u in range(PAIR):
-                bank = banks[(k, u)]
-                nc.vector.tensor_reduce(out=neg_max[:, u : u + 1], in_=bank[:], axis=AX.X, op=ALU.min)
-                e = work.tile([P, N], F32, name="exps")
-                nc.scalar.activation(
-                    out=e[:], in_=bank[:], func=ACT.Exp, bias=neg_max[:, u : u + 1], scale=-1.0,
-                    accum_out=total[:, u : u + 1],
-                )
-                exps[(k, u)] = e
-            totals[k] = total
+        def maximum_and_exp(k, u):
+            if u == 0:
+                neg_maxima[k] = small.tile([P, PAIR], F32, name="neg_max")
+                totals[k] = small.tile([P, PAIR], F32, name="total")
+            bank = banks[(k, u)]
+            nc.vector.tensor_reduce(out=neg_maxima[k][:, u : u + 1], in_=bank[:], axis=AX.X, op=ALU.min)
+            e = work.tile([P, N], F32, name="exps")
+            nc.scalar.activation(
+                out=e[:], in_=bank[:], func=ACT.Exp, bias=neg_maxima[k][:, u : u + 1], scale=-1.0,
+                accum_out=totals[k][:, u : u + 1],
+            )
+            exps[(k, u)] = e
 
         def reciprocals(k):
             inverse = small.tile([P, PAIR], F32, name="inverse")
@@ -169,21 +161,15 @@ def tile_softembedding_t_kernel(tc, input_numeric, proj_w, proj_b, emb_table, ou
                 )
                 weights[(k, u)] = w
 
-        def flip(k):
-            flipped = ps_flip.tile([P, PAIR, PACK, P], BF16, name="flipped")
-            for u in range(PAIR):
-                for c in range(PACK):
-                    nc.tensor.transpose(flipped[:, u, c, :], weights[(k, u)][:, c * P : (c + 1) * P], ident_bf16[:])
-            flips[k] = flipped
-
-        groupeds = {}
+        def flip(k, u):
+            if u == 0:
+                flips[k] = ps_flip.tile([P, PAIR, PACK, P], BF16, name="flipped")
+            for c in range(PACK):
+                nc.tensor.transpose(flips[k][:, u, c, :], weights[(k, u)][:, c * P : (c + 1) * P], ident_bf16[:])
 
         def group(k):
             grouped = quant.tile([P, PAIR, P, PACK], BF16, name="grouped", align_bytes=64)
-            if k < FILL:
-                nc.scalar.copy(out=grouped[:], in_=flips[k][:].rearrange("p u c t -> p u t c"))
-            else:
-                nc.vector.tensor_copy(out=grouped[:], in_=flips[k][:].rearrange("p u c t -> p u t c"))
+            nc.vector.tensor_copy(out=grouped[:], in_=flips[k][:].rearrange("p u c t -> p u t c"))
             groupeds[k] = grouped
 
         def quantise(k):
@@ -193,8 +179,6 @@ def tile_softembedding_t_kernel(tc, input_numeric, proj_w, proj_b, emb_table, ou
                 out=codes[:].bitcast(FP8X4), scales=scales[:], in_=groupeds[k][:].rearrange("p u t c -> p (u t c)")
             )
             packed[k] = (codes, scales)
-
-        accs = {}
 
         def passes(k):
             codes, scales = packed[k]
@@ -217,7 +201,7 @@ def tile_softembedding_t_kernel(tc, input_numeric, proj_w, proj_b, emb_table, ou
                 t0 = (k * PAIR + u) * P
                 result = store.tile([P, D], F32, name="result")
                 for h in range(D // HALF):
-                    if (u, h) in VECTOR_SHARE or (k >= PAIRS - TAIL and h == 0):
+                    if (u, h) in VECTOR_SHARE:
                         nc.vector.tensor_copy(out=result[:, h * HALF : (h + 1) * HALF], in_=accs[(k, u, h)][:])
                     else:
                         nc.scalar.copy(out=result[:, h * HALF : (h + 1) * HALF], in_=accs[(k, u, h)][:])
@@ -228,29 +212,33 @@ def tile_softembedding_t_kernel(tc, input_numeric, proj_w, proj_b, emb_table, ou
 
         with tc.manual_schedule():
             load_and_prepare()
-            logits(0)
-            for s in range(PAIRS + 4):
+            logits(0, 0)
+            logits(0, 1)
+            for s in range(PAIRS + 3):
+                if live(s - 3):
+                    quantise(s - 3)
+                    passes(s - 3)
+                if live(s - 1):
+                    normalise(s - 1)
+                    if s % BLOCK_PAIRS == 1 and (s + 3) // BLOCK_PAIRS < T // BLOCK:
+                        gpsimd_logits((s + 3) // BLOCK_PAIRS)
+                    flip(s - 1, 0)
                 if live(s):
-                    maxima_and_exps(s)
+                    maximum_and_exp(s, 0)
+                    maximum_and_exp(s, 1)
+                if live(s + 1):
+                    logits(s + 1, 0)
+                if live(s - 1):
+                    flip(s - 1, 1)
+                if live(s + 1):
+                    logits(s + 1, 1)
                 if s < 2:
                     regroup_table(s)
-                if live(s - 1):
-                    flip(s - 1)
                 if live(s - 3):
                     drain(s - 3)
-                if s == 2:
-                    quantise_table()
                 if live(s - 2):
-                    quantise(s - 2)
+                    group(s - 2)
                 if live(s):
                     reciprocals(s)
-                if live(s - 1):
-                    group(s - 1)
-                if live(s):
-                    normalise(s)
-                    if s % 4 == 1 and (s + 7) // 4 < len(BLOCKS):
-                        gpsimd_logits((s + 7) // 4)
-                if live(s + 1):
-                    logits(s + 1)
-                if live(s - 2):
-                    passes(s - 2)
+                if s == 2:
+                    quantise_table()

@@ -75,29 +75,31 @@ def tile_softembedding_t_kernel(tc, input_numeric, proj_w, proj_b, emb_table, ou
         accs = {}
 
         def load_and_prepare():
+            nc.gpsimd.memset(x_rows[:, 0:BLOCK].bitcast(F32), TWO_ONES)
             nc.vector.memset(wb_raw[:].bitcast(F32), 0.0)
-            nc.vector.memset(x_rows[:, 0:BLOCK].bitcast(F32), TWO_ONES)
             nc.sync.dma_start(out=wb_raw[0:1, :], in_=proj_w.rearrange("n o -> o n"))
             nc.sync.dma_start(out=wb_raw[ONES_ROW : ONES_ROW + 1, :], in_=proj_b.rearrange("(o n) -> o n", o=1))
             nc.sync.dma_start(out=x_rows[0:1, 0:BLOCK], in_=x_row[:, 0:BLOCK])
-            nc.scalar.dma_start(out=w4_raw[:], in_=proj_w.rearrange("(i c) o -> i (c o)", c=PACK))
-            nc.scalar.dma_start(out=b4_raw[:], in_=proj_b.rearrange("(i c) -> i c", c=PACK))
-            nc.gpsimd.memset(x_rows[:, BLOCK:T].bitcast(F32), TWO_ONES)
             nc.sync.dma_start(out=emb_raw[:], in_=emb_table.rearrange("(p j) d -> p j d", j=PACK))
+            nc.sync.dma_start(out=w4_raw[:], in_=proj_w.rearrange("(i c) o -> i (c o)", c=PACK))
+            nc.sync.dma_start(out=b4_raw[:], in_=proj_b.rearrange("(i c) -> i c", c=PACK))
+            nc.gpsimd.memset(x_rows[:, BLOCK:T].bitcast(F32), TWO_ONES)
             nc.sync.dma_start(out=x_rows[0:1, BLOCK:T], in_=x_row[:, BLOCK:T])
-            nc.scalar.dma_start(out=x_all[:, BLOCK:T], in_=x_flat[BLOCK:T].partition_broadcast(P))
+            nc.sync.dma_start(out=x_all[:, BLOCK:T], in_=x_flat[BLOCK:T].partition_broadcast(P))
             make_identity(nc, ident_bf16[:])
             make_identity(nc, ident_f32[:])
             nc.vector.tensor_scalar(
                 out=wb_neg[:], in0=wb_raw[:].rearrange("p (i c) -> p c i", c=PACK), scalar1=-1.0, scalar2=None,
                 op0=ALU.mult,
             )
+
+        def negate_last_chunk():
             nc.vector.tensor_scalar(out=neg_w4[:], in0=w4_raw[:], scalar1=-1.0, scalar2=None, op0=ALU.mult)
             nc.vector.tensor_scalar(out=neg_b4[:], in0=b4_raw[:], scalar1=-1.0, scalar2=None, op0=ALU.mult)
 
         def regroup_table(half):
             cols = slice(half * HALF, (half + 1) * HALF)
-            nc.scalar.copy(out=emb_grouped[:, cols, :], in_=emb_raw[:, :, cols].rearrange("p j d -> p d j"))
+            nc.vector.tensor_copy(out=emb_grouped[:, cols, :], in_=emb_raw[:, :, cols].rearrange("p j d -> p d j"))
 
         def quantise_table():
             nc.vector.quantize_mx(
@@ -201,7 +203,7 @@ def tile_softembedding_t_kernel(tc, input_numeric, proj_w, proj_b, emb_table, ou
                 t0 = (k * PAIR + u) * P
                 result = store.tile([P, D], F32, name="result")
                 for h in range(D // HALF):
-                    if (u, h) in VECTOR_SHARE:
+                    if (h == 0 and k == PAIRS - 1) or ((u, h) in VECTOR_SHARE and k % 2 == 0):
                         nc.vector.tensor_copy(out=result[:, h * HALF : (h + 1) * HALF], in_=accs[(k, u, h)][:])
                     else:
                         nc.scalar.copy(out=result[:, h * HALF : (h + 1) * HALF], in_=accs[(k, u, h)][:])
@@ -226,19 +228,21 @@ def tile_softembedding_t_kernel(tc, input_numeric, proj_w, proj_b, emb_table, ou
                 if live(s):
                     maximum_and_exp(s, 0)
                     maximum_and_exp(s, 1)
+                if s < 2:
+                    regroup_table(s)
+                if s == 0:
+                    negate_last_chunk()
+                if s == 2:
+                    quantise_table()
                 if live(s + 1):
                     logits(s + 1, 0)
                 if live(s - 1):
                     flip(s - 1, 1)
                 if live(s + 1):
                     logits(s + 1, 1)
-                if s < 2:
-                    regroup_table(s)
                 if live(s - 3):
                     drain(s - 3)
                 if live(s - 2):
                     group(s - 2)
                 if live(s):
                     reciprocals(s)
-                if s == 2:
-                    quantise_table()

@@ -25,6 +25,7 @@ BLOCK = 1024
 BLOCK_PAIRS = BLOCK // (P * PAIR)
 ONES_ROW = 32
 TWO_ONES = 1.0019378662109375
+TAIL = 2
 VECTOR_SHARE = ((0, 0),)
 
 FLOPS = 2 * T * N * D
@@ -157,10 +158,15 @@ def tile_softembedding_t_kernel(tc, input_numeric, proj_w, proj_b, emb_table, ou
         def normalise(k):
             for u in range(PAIR):
                 w = work.tile([P, N], BF16, name="weights")
-                nc.gpsimd.tensor_scalar(
-                    out=w[:], in0=exps[(k, u)][:], scalar1=inverses[k][:, u : u + 1], scalar2=0.0,
-                    op0=ALU.mult, op1=ALU.add,
-                )
+                if k == PAIRS - 1:
+                    nc.vector.tensor_scalar(
+                        out=w[:], in0=exps[(k, u)][:], scalar1=inverses[k][:, u : u + 1], scalar2=None, op0=ALU.mult
+                    )
+                else:
+                    nc.gpsimd.tensor_scalar(
+                        out=w[:], in0=exps[(k, u)][:], scalar1=inverses[k][:, u : u + 1], scalar2=0.0,
+                        op0=ALU.mult, op1=ALU.add,
+                    )
                 weights[(k, u)] = w
 
         def flip(k, u):
@@ -203,7 +209,7 @@ def tile_softembedding_t_kernel(tc, input_numeric, proj_w, proj_b, emb_table, ou
                 t0 = (k * PAIR + u) * P
                 result = store.tile([P, D], F32, name="result")
                 for h in range(D // HALF):
-                    if (h == 0 and k == PAIRS - 1) or ((u, h) in VECTOR_SHARE and k % 2 == 0):
+                    if (h == 0 and k >= PAIRS - TAIL) or ((u, h) in VECTOR_SHARE and k % 3 != 2):
                         nc.vector.tensor_copy(out=result[:, h * HALF : (h + 1) * HALF], in_=accs[(k, u, h)][:])
                     else:
                         nc.scalar.copy(out=result[:, h * HALF : (h + 1) * HALF], in_=accs[(k, u, h)][:])
@@ -224,7 +230,6 @@ def tile_softembedding_t_kernel(tc, input_numeric, proj_w, proj_b, emb_table, ou
                     normalise(s - 1)
                     if s % BLOCK_PAIRS == 1 and (s + 3) // BLOCK_PAIRS < T // BLOCK:
                         gpsimd_logits((s + 3) // BLOCK_PAIRS)
-                    flip(s - 1, 0)
                 if live(s):
                     maximum_and_exp(s, 0)
                     maximum_and_exp(s, 1)
@@ -234,15 +239,16 @@ def tile_softembedding_t_kernel(tc, input_numeric, proj_w, proj_b, emb_table, ou
                     negate_last_chunk()
                 if s == 2:
                     quantise_table()
-                if live(s + 1):
-                    logits(s + 1, 0)
-                if live(s - 1):
-                    flip(s - 1, 1)
-                if live(s + 1):
-                    logits(s + 1, 1)
+                for u in range(PAIR):
+                    if live(s + 1):
+                        logits(s + 1, u)
+                    if live(s - 1):
+                        flip(s - 1, u)
+                if s >= PAIRS and live(s - 2):
+                    group(s - 2)
                 if live(s - 3):
                     drain(s - 3)
-                if live(s - 2):
+                if s < PAIRS and live(s - 2):
                     group(s - 2)
                 if live(s):
                     reciprocals(s)

@@ -209,11 +209,15 @@ def tile_softembedding_t_kernel(tc, input_numeric, proj_w, proj_b, emb_table, ou
                 t0 = (k * PAIR + u) * P
                 result = store.tile([P, D], F32, name="result")
                 for h in range(D // HALF):
-                    if (h == 0 and k >= PAIRS - TAIL) or ((u, h) in VECTOR_SHARE and k % 3 != 2):
+                    if (h == 0 and k >= PAIRS - TAIL) or ((u, h) in VECTOR_SHARE and k % 2 == 0):
                         nc.vector.tensor_copy(out=result[:, h * HALF : (h + 1) * HALF], in_=accs[(k, u, h)][:])
                     else:
                         nc.scalar.copy(out=result[:, h * HALF : (h + 1) * HALF], in_=accs[(k, u, h)][:])
-                nc.sync.dma_start(out=out_rows[t0 : t0 + P, :], in_=result[:])
+                    if k == PAIRS - 1:
+                        cols = slice(h * HALF, (h + 1) * HALF)
+                        nc.sync.dma_start(out=out_rows[t0 : t0 + P, cols], in_=result[:, cols])
+                if k < PAIRS - 1:
+                    nc.sync.dma_start(out=out_rows[t0 : t0 + P, :], in_=result[:])
 
         def live(k):
             return 0 <= k < PAIRS

@@ -14,6 +14,7 @@ AX = mybir.AxisListType
 
 P = 128
 PACK = 4
+HALVES = 2
 T = 32 * 256
 N = 512
 D = 1024
@@ -51,18 +52,16 @@ def tile_softembedding_t_kernel(tc, input_numeric, proj_w, proj_b, emb_table, ou
         wb_raw = keep.tile([P, N], BF16)
         x_rows = keep.tile([P, T], BF16)
         x_all = keep.tile([P, T], BF16)
-        w4_raw = keep.tile([P, PACK], BF16)
-        b4_raw = keep.tile([P, PACK], BF16)
         emb_raw = keep.tile([P, PACK, D], BF16)
         ident_f32 = keep.tile([P, P], F32)
-        ident_bf16 = keep.tile([P, P], BF16)
-        wb_neg = keep.tile([P, PACK, P], BF16)
-        neg_w4 = keep.tile([P, PACK], F32)
-        neg_b4 = keep.tile([P, PACK], F32)
+        wb_neg = keep.tile([P, N], BF16)
+        wb_last = keep.tile([P, P], F32)
+        neg_last = keep.tile([P, 2], F32)
         emb_grouped = keep.tile([P, D, PACK], BF16, align_bytes=64)
         emb_codes = keep.tile([P, D], U32, align_bytes=64)
         emb_scales = keep.tile([P, D], U8, align_bytes=64)
 
+        corners = []
         last_chunk = {}
         banks = {}
         exps = {}
@@ -82,21 +81,24 @@ def tile_softembedding_t_kernel(tc, input_numeric, proj_w, proj_b, emb_table, ou
             nc.sync.dma_start(out=wb_raw[ONES_ROW : ONES_ROW + 1, :], in_=proj_b.rearrange("(o n) -> o n", o=1))
             nc.sync.dma_start(out=x_rows[0:1, 0:BLOCK], in_=x_row[:, 0:BLOCK])
             nc.sync.dma_start(out=emb_raw[:], in_=emb_table.rearrange("(p j) d -> p j d", j=PACK))
-            nc.sync.dma_start(out=w4_raw[:], in_=proj_w.rearrange("(i c) o -> i (c o)", c=PACK))
-            nc.sync.dma_start(out=b4_raw[:], in_=proj_b.rearrange("(i c) -> i c", c=PACK))
             nc.gpsimd.memset(x_rows[:, BLOCK:T].bitcast(F32), TWO_ONES)
             nc.sync.dma_start(out=x_rows[0:1, BLOCK:T], in_=x_row[:, BLOCK:T])
             nc.sync.dma_start(out=x_all[:, BLOCK:T], in_=x_flat[BLOCK:T].partition_broadcast(P))
-            make_identity(nc, ident_bf16[:])
             make_identity(nc, ident_f32[:])
             nc.vector.tensor_scalar(
-                out=wb_neg[:], in0=wb_raw[:].rearrange("p (i c) -> p c i", c=PACK), scalar1=-1.0, scalar2=None,
-                op0=ALU.mult,
+                out=wb_neg[:].rearrange("p (h i e) -> p h i e", h=HALVES, e=2),
+                in0=wb_raw[:].rearrange("p (i h e) -> p h i e", h=HALVES, e=2),
+                scalar1=-1.0, scalar2=None, op0=ALU.mult,
             )
+            nc.vector.tensor_copy(out=wb_last[:], in_=wb_neg[:, MM_CHUNKS * P : N])
 
-        def negate_last_chunk():
-            nc.vector.tensor_scalar(out=neg_w4[:], in0=w4_raw[:], scalar1=-1.0, scalar2=None, op0=ALU.mult)
-            nc.vector.tensor_scalar(out=neg_b4[:], in0=b4_raw[:], scalar1=-1.0, scalar2=None, op0=ALU.mult)
+        def flip_last_chunk():
+            corner = ps_flip.tile([P, P], F32, name="flipped")
+            nc.tensor.transpose(corner[:], wb_last[:], ident_f32[:])
+            corners.append(corner)
+
+        def keep_last_chunk():
+            nc.vector.tensor_copy(out=neg_last[:], in_=corners[0][:, 0 : 2 * ONES_ROW : ONES_ROW])
 
         def regroup_table(half):
             cols = slice(half * HALF, (half + 1) * HALF)
@@ -114,8 +116,8 @@ def tile_softembedding_t_kernel(tc, input_numeric, proj_w, proj_b, emb_table, ou
             nc.gpsimd.tensor_scalar(
                 out=tile[:],
                 in0=x_all[:, block * BLOCK : (block + 1) * BLOCK],
-                scalar1=neg_w4[:, MM_CHUNKS : MM_CHUNKS + 1],
-                scalar2=neg_b4[:, MM_CHUNKS : MM_CHUNKS + 1],
+                scalar1=neg_last[:, 0:1],
+                scalar2=neg_last[:, 1:2],
                 op0=ALU.mult,
                 op1=ALU.add,
             )
@@ -128,7 +130,7 @@ def tile_softembedding_t_kernel(tc, input_numeric, proj_w, proj_b, emb_table, ou
             nc.tensor.matmul(
                 out=bank[:, 0 : chunks * P],
                 lhsT=x_rows[:, t0 : t0 + P],
-                rhs=wb_neg[:, 0:chunks, :].rearrange("p c i -> p (c i)"),
+                rhs=wb_neg[:, 0 : chunks * P],
                 start=True,
                 stop=True,
             )
@@ -171,13 +173,14 @@ def tile_softembedding_t_kernel(tc, input_numeric, proj_w, proj_b, emb_table, ou
 
         def flip(k, u):
             if u == 0:
-                flips[k] = ps_flip.tile([P, PAIR, PACK, P], BF16, name="flipped")
-            for c in range(PACK):
-                nc.tensor.transpose(flips[k][:, u, c, :], weights[(k, u)][:, c * P : (c + 1) * P], ident_bf16[:])
+                flips[k] = ps_flip.tile([P, PAIR, HALVES, P], F32, name="flipped")
+            words = weights[(k, u)][:].bitcast(F32)
+            for h in range(HALVES):
+                nc.tensor.transpose(flips[k][:, u, h, :], words[:, h * P : (h + 1) * P], ident_f32[:])
 
         def group(k):
             grouped = quant.tile([P, PAIR, P, PACK], BF16, name="grouped", align_bytes=64)
-            nc.vector.tensor_copy(out=grouped[:], in_=flips[k][:].rearrange("p u c t -> p u t c"))
+            nc.vector.tensor_copy(out=grouped[:].bitcast(F32), in_=flips[k][:].rearrange("p u h t -> p u t h"))
             groupeds[k] = grouped
 
         def quantise(k):
@@ -209,7 +212,7 @@ def tile_softembedding_t_kernel(tc, input_numeric, proj_w, proj_b, emb_table, ou
                 t0 = (k * PAIR + u) * P
                 result = store.tile([P, D], F32, name="result")
                 for h in range(D // HALF):
-                    if (h == 0 and k >= PAIRS - TAIL) or ((u, h) in VECTOR_SHARE and k % 2 == 0):
+                    if (h == 0 and k >= PAIRS - TAIL) or (u, h) in VECTOR_SHARE:
                         nc.vector.tensor_copy(out=result[:, h * HALF : (h + 1) * HALF], in_=accs[(k, u, h)][:])
                     else:
                         nc.scalar.copy(out=result[:, h * HALF : (h + 1) * HALF], in_=accs[(k, u, h)][:])
@@ -226,6 +229,7 @@ def tile_softembedding_t_kernel(tc, input_numeric, proj_w, proj_b, emb_table, ou
             load_and_prepare()
             logits(0, 0)
             logits(0, 1)
+            flip_last_chunk()
             for s in range(PAIRS + 3):
                 if live(s - 3):
                     quantise(s - 3)
@@ -240,7 +244,7 @@ def tile_softembedding_t_kernel(tc, input_numeric, proj_w, proj_b, emb_table, ou
                 if s < 2:
                     regroup_table(s)
                 if s == 0:
-                    negate_last_chunk()
+                    keep_last_chunk()
                 if s == 2:
                     quantise_table()
                 for u in range(PAIR):

@@ -23,7 +23,6 @@ PAIR = 2
 PAIRS = T // (P * PAIR)
 MM_CHUNKS = 3
 BLOCK = 1024
-BLOCK_PAIRS = BLOCK // (P * PAIR)
 ONES_ROW = 32
 TWO_ONES = 1.0019378662109375
 TAIL = 2
@@ -40,7 +39,7 @@ def tile_softembedding_t_kernel(tc, input_numeric, proj_w, proj_b, emb_table, ou
 
     with ExitStack() as ctx:
         keep = ctx.enter_context(tc.tile_pool(name="keep", bufs=1))
-        logit_pool = ctx.enter_context(tc.tile_pool(name="logit", bufs=2))
+        logit_pool = ctx.enter_context(tc.tile_pool(name="logit", bufs=4))
         work = ctx.enter_context(tc.tile_pool(name="work", bufs=6))
         small = ctx.enter_context(tc.tile_pool(name="small", bufs=6))
         quant = ctx.enter_context(tc.tile_pool(name="quant", bufs=3))
@@ -111,17 +110,17 @@ def tile_softembedding_t_kernel(tc, input_numeric, proj_w, proj_b, emb_table, ou
                 in_=emb_grouped[:].rearrange("p d j -> p (d j)"),
             )
 
-        def gpsimd_logits(block):
-            tile = logit_pool.tile([P, BLOCK], F32, name="neg_last")
+        def gpsimd_logits(k):
+            tile = logit_pool.tile([P, PAIR * P], F32, name="neg_last")
             nc.gpsimd.tensor_scalar(
                 out=tile[:],
-                in0=x_all[:, block * BLOCK : (block + 1) * BLOCK],
+                in0=x_all[:, k * PAIR * P : (k + 1) * PAIR * P],
                 scalar1=neg_last[:, 0:1],
                 scalar2=neg_last[:, 1:2],
                 op0=ALU.mult,
                 op1=ALU.add,
             )
-            last_chunk[block] = tile
+            last_chunk[k] = tile
 
         def logits(k, u):
             t0 = (k * PAIR + u) * P
@@ -135,8 +134,7 @@ def tile_softembedding_t_kernel(tc, input_numeric, proj_w, proj_b, emb_table, ou
                 stop=True,
             )
             if chunks < PACK:
-                at = t0 % BLOCK
-                nc.tensor.transpose(bank[:, MM_CHUNKS * P : N], last_chunk[t0 // BLOCK][:, at : at + P], ident_f32[:])
+                nc.tensor.transpose(bank[:, MM_CHUNKS * P : N], last_chunk[k][:, u * P : (u + 1) * P], ident_f32[:])
             banks[(k, u)] = bank
 
         def maximum_and_exp(k, u):
@@ -236,8 +234,8 @@ def tile_softembedding_t_kernel(tc, input_numeric, proj_w, proj_b, emb_table, ou
                     passes(s - 3)
                 if live(s - 1):
                     normalise(s - 1)
-                    if s % BLOCK_PAIRS == 1 and (s + 3) // BLOCK_PAIRS < T // BLOCK:
-                        gpsimd_logits((s + 3) // BLOCK_PAIRS)
+                if live(s + 2) and (s + 2) * PAIR * P >= BLOCK:
+                    gpsimd_logits(s + 2)
                 if live(s):
                     maximum_and_exp(s, 0)
                     maximum_and_exp(s, 1)

@@ -250,11 +250,9 @@ def tile_softembedding_t_kernel(tc, input_numeric, proj_w, proj_b, emb_table, ou
                         logits(s + 1, u)
                     if live(s - 1):
                         flip(s - 1, u)
-                if s >= PAIRS and live(s - 2):
+                if live(s - 2):
                     group(s - 2)
                 if live(s - 3):
                     drain(s - 3)
-                if s < PAIRS and live(s - 2):
-                    group(s - 2)
                 if live(s):
                     reciprocals(s)

@@ -110,9 +110,9 @@ def tile_softembedding_t_kernel(tc, input_numeric, proj_w, proj_b, emb_table, ou
                 in_=emb_grouped[:].rearrange("p d j -> p (d j)"),
             )
 
-        def gpsimd_logits(k):
+        def last_chunk_logits(k):
             tile = logit_pool.tile([P, PAIR * P], F32, name="neg_last")
-            nc.gpsimd.tensor_scalar(
+            nc.vector.tensor_scalar(
                 out=tile[:],
                 in0=x_all[:, k * PAIR * P : (k + 1) * PAIR * P],
                 scalar1=neg_last[:, 0:1],
@@ -234,8 +234,6 @@ def tile_softembedding_t_kernel(tc, input_numeric, proj_w, proj_b, emb_table, ou
                     passes(s - 3)
                 if live(s - 1):
                     normalise(s - 1)
-                if live(s + 2) and (s + 2) * PAIR * P >= BLOCK:
-                    gpsimd_logits(s + 2)
                 if live(s):
                     maximum_and_exp(s, 0)
                     maximum_and_exp(s, 1)
@@ -254,5 +252,7 @@ def tile_softembedding_t_kernel(tc, input_numeric, proj_w, proj_b, emb_table, ou
                     group(s - 2)
                 if live(s - 3):
                     drain(s - 3)
+                if live(s + 2) and (s + 2) * PAIR * P >= BLOCK:
+                    last_chunk_logits(s + 2)
                 if live(s):
                     reciprocals(s)

@@ -74,16 +74,17 @@ def tile_softembedding_t_kernel(tc, input_numeric, proj_w, proj_b, emb_table, ou
         accs = {}
 
         def load_and_prepare():
+            nc.gpsimd.memset(wb_raw[:].bitcast(F32), 0.0)
             nc.gpsimd.memset(x_rows[:, 0:BLOCK].bitcast(F32), TWO_ONES)
-            nc.vector.memset(wb_raw[:].bitcast(F32), 0.0)
             nc.sync.dma_start(out=wb_raw[0:1, :], in_=proj_w.rearrange("n o -> o n"))
             nc.sync.dma_start(out=wb_raw[ONES_ROW : ONES_ROW + 1, :], in_=proj_b.rearrange("(o n) -> o n", o=1))
             nc.sync.dma_start(out=x_rows[0:1, 0:BLOCK], in_=x_row[:, 0:BLOCK])
             nc.sync.dma_start(out=emb_raw[:], in_=emb_table.rearrange("(p j) d -> p j d", j=PACK))
-            nc.gpsimd.memset(x_rows[:, BLOCK:T].bitcast(F32), TWO_ONES)
-            nc.sync.dma_start(out=x_rows[0:1, BLOCK:T], in_=x_row[:, BLOCK:T])
-            nc.sync.dma_start(out=x_all[:, BLOCK:T], in_=x_flat[BLOCK:T].partition_broadcast(P))
             make_identity(nc, ident_f32[:])
+            for t0 in range(BLOCK, T, BLOCK):
+                nc.gpsimd.memset(x_rows[:, t0 : t0 + BLOCK].bitcast(F32), TWO_ONES)
+            nc.sync.dma_start(out=x_all[:, BLOCK:T], in_=x_flat[BLOCK:T].partition_broadcast(P))
+            nc.sync.dma_start(out=x_rows[0:1, BLOCK:T], in_=x_row[:, BLOCK:T])
             nc.vector.tensor_scalar(
                 out=wb_neg[:].rearrange("p (h i e) -> p h i e", h=HALVES, e=2),
                 in0=wb_raw[:].rearrange("p (i h e) -> p h i e", h=HALVES, e=2),

@@ -23,6 +23,7 @@ PAIR = 2
 PAIRS = T // (P * PAIR)
 MM_CHUNKS = 3
 BLOCK = 1024
+SHARED_PAIRS = 2
 ONES_ROW = 32
 TWO_ONES = 1.0019378662109375
 TAIL = 2
@@ -56,6 +57,7 @@ def tile_softembedding_t_kernel(tc, input_numeric, proj_w, proj_b, emb_table, ou
         wb_neg = keep.tile([P, N], BF16)
         wb_last = keep.tile([P, P], F32)
         neg_last = keep.tile([P, 2], F32)
+        warm = keep.tile([P, 1], F32)
         emb_grouped = keep.tile([P, D, PACK], BF16, align_bytes=64)
         emb_codes = keep.tile([P, D], U32, align_bytes=64)
         emb_scales = keep.tile([P, D], U8, align_bytes=64)
@@ -80,17 +82,26 @@ def tile_softembedding_t_kernel(tc, input_numeric, proj_w, proj_b, emb_table, ou
             nc.sync.dma_start(out=wb_raw[ONES_ROW : ONES_ROW + 1, :], in_=proj_b.rearrange("(o n) -> o n", o=1))
             nc.sync.dma_start(out=x_rows[0:1, 0:BLOCK], in_=x_row[:, 0:BLOCK])
             nc.sync.dma_start(out=emb_raw[:], in_=emb_table.rearrange("(p j) d -> p j d", j=PACK))
+            nc.gpsimd.memset(x_rows[:, BLOCK : 2 * BLOCK].bitcast(F32), TWO_ONES)
             make_identity(nc, ident_f32[:])
-            for t0 in range(BLOCK, T, BLOCK):
-                nc.gpsimd.memset(x_rows[:, t0 : t0 + BLOCK].bitcast(F32), TWO_ONES)
+            nc.gpsimd.memset(x_rows[:, 2 * BLOCK : 3 * BLOCK].bitcast(F32), TWO_ONES)
             nc.sync.dma_start(out=x_all[:, BLOCK:T], in_=x_flat[BLOCK:T].partition_broadcast(P))
-            nc.sync.dma_start(out=x_rows[0:1, BLOCK:T], in_=x_row[:, BLOCK:T])
+            nc.scalar.activation(out=warm[:], in_=x_rows[:, BLOCK : BLOCK + 2].bitcast(F32), func=ACT.Exp)
+            for t0 in range(3 * BLOCK, T - BLOCK, BLOCK):
+                copy_ones(t0)
             nc.vector.tensor_scalar(
                 out=wb_neg[:].rearrange("p (h i e) -> p h i e", h=HALVES, e=2),
                 in0=wb_raw[:].rearrange("p (i h e) -> p h i e", h=HALVES, e=2),
                 scalar1=-1.0, scalar2=None, op0=ALU.mult,
             )
             nc.vector.tensor_copy(out=wb_last[:], in_=wb_neg[:, MM_CHUNKS * P : N])
+
+        def copy_ones(t0):
+            nc.scalar.copy(out=x_rows[:, t0 : t0 + BLOCK].bitcast(F32), in_=x_rows[:, BLOCK : 2 * BLOCK].bitcast(F32))
+
+        def last_ones_and_x():
+            copy_ones(T - BLOCK)
+            nc.sync.dma_start(out=x_rows[0:1, BLOCK:T], in_=x_row[:, BLOCK:T])
 
         def flip_last_chunk():
             corner = ps_flip.tile([P, P], F32, name="flipped")
@@ -159,7 +170,9 @@ def tile_softembedding_t_kernel(tc, input_numeric, proj_w, proj_b, emb_table, ou
         def normalise(k):
             for u in range(PAIR):
                 w = work.tile([P, N], BF16, name="weights")
-                if k == PAIRS - 1:
+                if k < SHARED_PAIRS and u == 1:
+                    nc.scalar.activation(out=w[:], in_=exps[(k, u)][:], func=ACT.Copy, scale=inverses[k][:, u : u + 1])
+                elif k == PAIRS - 1:
                     nc.vector.tensor_scalar(
                         out=w[:], in0=exps[(k, u)][:], scalar1=inverses[k][:, u : u + 1], scalar2=None, op0=ALU.mult
                     )
@@ -238,6 +251,8 @@ def tile_softembedding_t_kernel(tc, input_numeric, proj_w, proj_b, emb_table, ou
                 if live(s):
                     maximum_and_exp(s, 0)
                     maximum_and_exp(s, 1)
+                if s == 0:
+                    last_ones_and_x()
                 if s < 2:
                     regroup_table(s)
                 if s == 0:

@@ -29,6 +29,9 @@ TWO_ONES = 1.0019378662109375
 TAIL = 2
 VECTOR_SHARE = ((0, 0),)
 
+SPLIT_BANK = (1, 1)
+SLICE = 128
+
 FLOPS = 2 * T * N * D
 
 
@@ -124,7 +127,7 @@ def tile_softembedding_t_kernel(tc, input_numeric, proj_w, proj_b, emb_table, ou
 
         def last_chunk_logits(k):
             tile = logit_pool.tile([P, PAIR * P], F32, name="neg_last")
-            nc.vector.tensor_scalar(
+            nc.gpsimd.tensor_scalar(
                 out=tile[:],
                 in0=x_all[:, k * PAIR * P : (k + 1) * PAIR * P],
                 scalar1=neg_last[:, 0:1],
@@ -226,6 +229,10 @@ def tile_softembedding_t_kernel(tc, input_numeric, proj_w, proj_b, emb_table, ou
                 for h in range(D // HALF):
                     if (h == 0 and k >= PAIRS - TAIL) or (u, h) in VECTOR_SHARE:
                         nc.vector.tensor_copy(out=result[:, h * HALF : (h + 1) * HALF], in_=accs[(k, u, h)][:])
+                    elif (u, h) == SPLIT_BANK and k < PAIRS - TAIL:
+                        cut = h * HALF + SLICE
+                        nc.vector.tensor_copy(out=result[:, h * HALF : cut], in_=accs[(k, u, h)][:, 0:SLICE])
+                        nc.scalar.copy(out=result[:, cut : (h + 1) * HALF], in_=accs[(k, u, h)][:, SLICE:HALF])
                     else:
                         nc.scalar.copy(out=result[:, h * HALF : (h + 1) * HALF], in_=accs[(k, u, h)][:])
                     if k == PAIRS - 1:
@@ -248,6 +255,8 @@ def tile_softembedding_t_kernel(tc, input_numeric, proj_w, proj_b, emb_table, ou
                     passes(s - 3)
                 if live(s - 1):
                     normalise(s - 1)
+                if live(s + 2) and (s + 2) * PAIR * P >= BLOCK:
+                    last_chunk_logits(s + 2)
                 if live(s):
                     maximum_and_exp(s, 0)
                     maximum_and_exp(s, 1)
@@ -268,7 +277,5 @@ def tile_softembedding_t_kernel(tc, input_numeric, proj_w, proj_b, emb_table, ou
                     group(s - 2)
                 if live(s - 3):
                     drain(s - 3)
-                if live(s + 2) and (s + 2) * PAIR * P >= BLOCK:
-                    last_chunk_logits(s + 2)
                 if live(s):
                     reciprocals(s)

@@ -24,7 +24,10 @@ PAIRS = T // (P * PAIR)
 MM_CHUNKS = 3
 BLOCK = 1024
 SHARED_PAIRS = 2
-ONES_ROW = 32
+ONES_ROW = 1
+EARLY_COPIES = 2
+LATE_COPIES = 3
+FIRST = 2 * PAIR * P
 TWO_ONES = 1.0019378662109375
 TAIL = 2
 VECTOR_SHARE = ((0, 0),)
@@ -79,32 +82,34 @@ def tile_softembedding_t_kernel(tc, input_numeric, proj_w, proj_b, emb_table, ou
         accs = {}
 
         def load_and_prepare():
-            nc.gpsimd.memset(wb_raw[:].bitcast(F32), 0.0)
-            nc.gpsimd.memset(x_rows[:, 0:BLOCK].bitcast(F32), TWO_ONES)
             nc.sync.dma_start(out=wb_raw[0:1, :], in_=proj_w.rearrange("n o -> o n"))
             nc.sync.dma_start(out=wb_raw[ONES_ROW : ONES_ROW + 1, :], in_=proj_b.rearrange("(o n) -> o n", o=1))
-            nc.sync.dma_start(out=x_rows[0:1, 0:BLOCK], in_=x_row[:, 0:BLOCK])
+            nc.gpsimd.memset(x_rows[:, 0:FIRST].bitcast(F32), TWO_ONES)
+            nc.sync.dma_start(out=x_rows[0:1, 0:FIRST], in_=x_row[:, 0:FIRST])
             nc.sync.dma_start(out=emb_raw[:], in_=emb_table.rearrange("(p j) d -> p j d", j=PACK))
-            nc.gpsimd.memset(x_rows[:, BLOCK : 2 * BLOCK].bitcast(F32), TWO_ONES)
+            nc.gpsimd.memset(wb_neg[:].bitcast(F32), 0.0)
+            nc.gpsimd.memset(x_rows[:, FIRST:BLOCK].bitcast(F32), TWO_ONES)
+            nc.sync.dma_start(out=x_rows[0:1, FIRST:BLOCK], in_=x_row[:, FIRST:BLOCK])
+            nc.gpsimd.memset(x_rows[:, T - BLOCK : T].bitcast(F32), TWO_ONES)
             make_identity(nc, ident_f32[:])
-            nc.gpsimd.memset(x_rows[:, 2 * BLOCK : 3 * BLOCK].bitcast(F32), TWO_ONES)
+            nc.scalar.activation(out=warm[:], in_=x_rows[:, T - BLOCK : T - BLOCK + 2].bitcast(F32), func=ACT.Exp)
             nc.sync.dma_start(out=x_all[:, BLOCK:T], in_=x_flat[BLOCK:T].partition_broadcast(P))
-            nc.scalar.activation(out=warm[:], in_=x_rows[:, BLOCK : BLOCK + 2].bitcast(F32), func=ACT.Exp)
-            for t0 in range(3 * BLOCK, T - BLOCK, BLOCK):
+            copy_ones(BLOCK)
+            nc.sync.dma_start(out=x_rows[0:1, BLOCK : 2 * BLOCK], in_=x_row[:, BLOCK : 2 * BLOCK])
+            for t0 in range(2 * BLOCK, (2 + EARLY_COPIES) * BLOCK, BLOCK):
                 copy_ones(t0)
             nc.vector.tensor_scalar(
-                out=wb_neg[:].rearrange("p (h i e) -> p h i e", h=HALVES, e=2),
-                in0=wb_raw[:].rearrange("p (i h e) -> p h i e", h=HALVES, e=2),
+                out=wb_neg[0 : ONES_ROW + 1, :].rearrange("p (h i e) -> p h i e", h=HALVES, e=2),
+                in0=wb_raw[0 : ONES_ROW + 1, :].rearrange("p (i h e) -> p h i e", h=HALVES, e=2),
                 scalar1=-1.0, scalar2=None, op0=ALU.mult,
             )
             nc.vector.tensor_copy(out=wb_last[:], in_=wb_neg[:, MM_CHUNKS * P : N])
 
         def copy_ones(t0):
-            nc.scalar.copy(out=x_rows[:, t0 : t0 + BLOCK].bitcast(F32), in_=x_rows[:, BLOCK : 2 * BLOCK].bitcast(F32))
+            nc.scalar.copy(out=x_rows[:, t0 : t0 + BLOCK].bitcast(F32), in_=x_rows[:, T - BLOCK : T].bitcast(F32))
 
-        def last_ones_and_x():
-            copy_ones(T - BLOCK)
-            nc.sync.dma_start(out=x_rows[0:1, BLOCK:T], in_=x_row[:, BLOCK:T])
+        def load_other_x():
+            nc.sync.dma_start(out=x_rows[0:1, 2 * BLOCK : T], in_=x_row[:, 2 * BLOCK : T])
 
         def flip_last_chunk():
             corner = ps_flip.tile([P, P], F32, name="flipped")
@@ -260,8 +265,10 @@ def tile_softembedding_t_kernel(tc, input_numeric, proj_w, proj_b, emb_table, ou
                 if live(s):
                     maximum_and_exp(s, 0)
                     maximum_and_exp(s, 1)
-                if s == 0:
-                    last_ones_and_x()
+                if s < LATE_COPIES:
+                    copy_ones((2 + EARLY_COPIES + s) * BLOCK)
+                if s == LATE_COPIES - 1:
+                    load_other_x()
                 if s < 2:
                     regroup_table(s)
                 if s == 0:

@@ -23,10 +23,11 @@ PAIR = 2
 PAIRS = T // (P * PAIR)
 MM_CHUNKS = 3
 BLOCK = 1024
-SHARED_PAIRS = 2
+STEPS_A_BLOCK = BLOCK // (P * PAIR)
+EARLY = 3
+QUARTER = 256
+ROW_TILES = 2
 ONES_ROW = 1
-EARLY_COPIES = 2
-LATE_COPIES = 3
 FIRST = 2 * PAIR * P
 TWO_ONES = 1.0019378662109375
 TAIL = 2
@@ -56,9 +57,9 @@ def tile_softembedding_t_kernel(tc, input_numeric, proj_w, proj_b, emb_table, ou
         ps_out = ctx.enter_context(tc.psum_pool(name="ps_out", bufs=4))
 
         wb_raw = keep.tile([P, N], BF16)
-        x_rows = keep.tile([P, T], BF16)
+        x_rows = [keep.tile([P, BLOCK], BF16, name="x_rows_%d" % i) for i in range(ROW_TILES)]
         x_all = keep.tile([P, T], BF16)
-        emb_raw = keep.tile([P, PACK, D], BF16)
+        emb_raw = [keep.tile([P, PACK, HALF], BF16, name="emb_raw_%d" % h) for h in range(D // HALF)]
         ident_f32 = keep.tile([P, P], F32)
         wb_neg = keep.tile([P, N], BF16)
         wb_last = keep.tile([P, P], F32)
@@ -84,20 +85,20 @@ def tile_softembedding_t_kernel(tc, input_numeric, proj_w, proj_b, emb_table, ou
         def load_and_prepare():
             nc.sync.dma_start(out=wb_raw[0:1, :], in_=proj_w.rearrange("n o -> o n"))
             nc.sync.dma_start(out=wb_raw[ONES_ROW : ONES_ROW + 1, :], in_=proj_b.rearrange("(o n) -> o n", o=1))
-            nc.gpsimd.memset(x_rows[:, 0:FIRST].bitcast(F32), TWO_ONES)
-            nc.sync.dma_start(out=x_rows[0:1, 0:FIRST], in_=x_row[:, 0:FIRST])
-            nc.sync.dma_start(out=emb_raw[:], in_=emb_table.rearrange("(p j) d -> p j d", j=PACK))
+            nc.gpsimd.memset(x_rows[0][:, 0:FIRST].bitcast(F32), TWO_ONES)
+            nc.sync.dma_start(out=x_rows[0][0:1, 0:FIRST], in_=x_row[:, 0:FIRST])
+            for h in range(D // HALF):
+                cols = slice(h * HALF, (h + 1) * HALF)
+                nc.sync.dma_start(out=emb_raw[h][:], in_=emb_table[:, cols].rearrange("(p j) d -> p j d", j=PACK))
             nc.gpsimd.memset(wb_neg[:].bitcast(F32), 0.0)
-            nc.gpsimd.memset(x_rows[:, FIRST:BLOCK].bitcast(F32), TWO_ONES)
-            nc.sync.dma_start(out=x_rows[0:1, FIRST:BLOCK], in_=x_row[:, FIRST:BLOCK])
-            nc.gpsimd.memset(x_rows[:, T - BLOCK : T].bitcast(F32), TWO_ONES)
+            nc.gpsimd.memset(x_rows[0][:, FIRST:BLOCK].bitcast(F32), TWO_ONES)
+            nc.sync.dma_start(out=x_rows[0][0:1, FIRST:BLOCK], in_=x_row[:, FIRST:BLOCK])
+            nc.gpsimd.memset(x_rows[1][:].bitcast(F32), TWO_ONES)
             make_identity(nc, ident_f32[:])
-            nc.scalar.activation(out=warm[:], in_=x_rows[:, T - BLOCK : T - BLOCK + 2].bitcast(F32), func=ACT.Exp)
-            nc.sync.dma_start(out=x_all[:, BLOCK:T], in_=x_flat[BLOCK:T].partition_broadcast(P))
-            copy_ones(BLOCK)
-            nc.sync.dma_start(out=x_rows[0:1, BLOCK : 2 * BLOCK], in_=x_row[:, BLOCK : 2 * BLOCK])
-            for t0 in range(2 * BLOCK, (2 + EARLY_COPIES) * BLOCK, BLOCK):
-                copy_ones(t0)
+            nc.scalar.activation(out=warm[:], in_=x_rows[1][:, 0:2].bitcast(F32), func=ACT.Exp)
+            for t0, t1 in ((BLOCK, 2 * BLOCK), (2 * BLOCK, T)):
+                nc.sync.dma_start(out=x_all[:, t0:t1], in_=x_flat[t0:t1].partition_broadcast(P))
+            load_x_row(1)
             nc.vector.tensor_scalar(
                 out=wb_neg[0 : ONES_ROW + 1, :].rearrange("p (h i e) -> p h i e", h=HALVES, e=2),
                 in0=wb_raw[0 : ONES_ROW + 1, :].rearrange("p (i h e) -> p h i e", h=HALVES, e=2),
@@ -105,11 +106,9 @@ def tile_softembedding_t_kernel(tc, input_numeric, proj_w, proj_b, emb_table, ou
             )
             nc.vector.tensor_copy(out=wb_last[:], in_=wb_neg[:, MM_CHUNKS * P : N])
 
-        def copy_ones(t0):
-            nc.scalar.copy(out=x_rows[:, t0 : t0 + BLOCK].bitcast(F32), in_=x_rows[:, T - BLOCK : T].bitcast(F32))
-
-        def load_other_x():
-            nc.sync.dma_start(out=x_rows[0:1, 2 * BLOCK : T], in_=x_row[:, 2 * BLOCK : T])
+        def load_x_row(block):
+            t0 = block * BLOCK
+            nc.sync.dma_start(out=x_rows[block % ROW_TILES][0:1, :], in_=x_row[:, t0 : t0 + BLOCK])
 
         def flip_last_chunk():
             corner = ps_flip.tile([P, P], F32, name="flipped")
@@ -119,15 +118,23 @@ def tile_softembedding_t_kernel(tc, input_numeric, proj_w, proj_b, emb_table, ou
         def keep_last_chunk():
             nc.vector.tensor_copy(out=neg_last[:], in_=corners[0][:, 0 : 2 * ONES_ROW : ONES_ROW])
 
-        def regroup_table(half):
-            cols = slice(half * HALF, (half + 1) * HALF)
-            nc.vector.tensor_copy(out=emb_grouped[:, cols, :], in_=emb_raw[:, :, cols].rearrange("p j d -> p d j"))
+        def regroup_table(engine, quarter):
+            first = quarter % 2 * QUARTER
+            target = emb_grouped[:, quarter * QUARTER : (quarter + 1) * QUARTER, :]
+            source = emb_raw[quarter // 2][:, :, first : first + QUARTER].rearrange("p j d -> p d j")
+            if engine == "gpsimd":
+                nc.gpsimd.tensor_scalar(out=target, in0=source, scalar1=1.0, scalar2=0.0, op0=ALU.mult, op1=ALU.add)
+            elif engine == "scalar":
+                nc.scalar.copy(out=target, in_=source)
+            else:
+                nc.vector.tensor_copy(out=target, in_=source)
 
-        def quantise_table():
+        def quantise_table(half):
+            cols = slice(half * HALF, (half + 1) * HALF)
             nc.vector.quantize_mx(
-                out=emb_codes[:].bitcast(FP8X4),
-                scales=emb_scales[:],
-                in_=emb_grouped[:].rearrange("p d j -> p (d j)"),
+                out=emb_codes[:, cols].bitcast(FP8X4),
+                scales=emb_scales[:, cols],
+                in_=emb_grouped[:, cols, :].rearrange("p d j -> p (d j)"),
             )
 
         def last_chunk_logits(k):
@@ -143,12 +150,13 @@ def tile_softembedding_t_kernel(tc, input_numeric, proj_w, proj_b, emb_table, ou
             last_chunk[k] = tile
 
         def logits(k, u):
+            spare = 0 < k < EARLY
             t0 = (k * PAIR + u) * P
             chunks = PACK if t0 < BLOCK else MM_CHUNKS
-            bank = ps_logit.tile([P, N], F32, name="bank")
+            bank = ps_out.tile([P, N], F32, name="acc") if spare else ps_logit.tile([P, N], F32, name="bank")
             nc.tensor.matmul(
                 out=bank[:, 0 : chunks * P],
-                lhsT=x_rows[:, t0 : t0 + P],
+                lhsT=x_rows[t0 // BLOCK % ROW_TILES][:, t0 % BLOCK : t0 % BLOCK + P],
                 rhs=wb_neg[:, 0 : chunks * P],
                 start=True,
                 stop=True,
@@ -175,10 +183,10 @@ def tile_softembedding_t_kernel(tc, input_numeric, proj_w, proj_b, emb_table, ou
             nc.vector.reciprocal(out=inverse[:], in_=totals[k][:])
             inverses[k] = inverse
 
-        def normalise(k):
-            for u in range(PAIR):
+        def normalise(k, tiles=(0, 1), engine="gpsimd"):
+            for u in tiles:
                 w = work.tile([P, N], BF16, name="weights")
-                if k < SHARED_PAIRS and u == 1:
+                if engine == "scalar":
                     nc.scalar.activation(out=w[:], in_=exps[(k, u)][:], func=ACT.Copy, scale=inverses[k][:, u : u + 1])
                 elif k == PAIRS - 1:
                     nc.vector.tensor_scalar(
@@ -246,43 +254,73 @@ def tile_softembedding_t_kernel(tc, input_numeric, proj_w, proj_b, emb_table, ou
                 if k < PAIRS - 1:
                     nc.sync.dma_start(out=out_rows[t0 : t0 + P, :], in_=result[:])
 
-        def live(k):
-            return 0 <= k < PAIRS
-
-        with tc.manual_schedule():
-            load_and_prepare()
+        def start():
             logits(0, 0)
             logits(0, 1)
             flip_last_chunk()
-            for s in range(PAIRS + 3):
-                if live(s - 3):
-                    quantise(s - 3)
-                    passes(s - 3)
-                if live(s - 1):
-                    normalise(s - 1)
-                if live(s + 2) and (s + 2) * PAIR * P >= BLOCK:
-                    last_chunk_logits(s + 2)
-                if live(s):
-                    maximum_and_exp(s, 0)
-                    maximum_and_exp(s, 1)
-                if s < LATE_COPIES:
-                    copy_ones((2 + EARLY_COPIES + s) * BLOCK)
-                if s == LATE_COPIES - 1:
-                    load_other_x()
-                if s < 2:
-                    regroup_table(s)
-                if s == 0:
-                    keep_last_chunk()
-                if s == 2:
-                    quantise_table()
-                for u in range(PAIR):
-                    if live(s + 1):
-                        logits(s + 1, u)
-                    if live(s - 1):
-                        flip(s - 1, u)
-                if live(s - 2):
-                    group(s - 2)
-                if live(s - 3):
-                    drain(s - 3)
-                if live(s):
-                    reciprocals(s)
+            for k in range(1, EARLY):
+                logits(k, 0)
+                logits(k, 1)
+            regroup_table("gpsimd", 0)
+            regroup_table("gpsimd", 1)
+            maximum_and_exp(0, 0)
+            maximum_and_exp(0, 1)
+            keep_last_chunk()
+            maximum_and_exp(1, 0)
+            maximum_and_exp(1, 1)
+            reciprocals(0)
+            normalise(0, engine="scalar")
+            logits(EARLY, 0)
+            logits(EARLY, 1)
+            maximum_and_exp(2, 0)
+            maximum_and_exp(2, 1)
+            regroup_table("scalar", 3)
+            reciprocals(1)
+            flip(0, 0)
+            flip(0, 1)
+            normalise(1)
+            last_chunk_logits(EARLY + 1)
+            regroup_table("vector", 2)
+            maximum_and_exp(EARLY, 0)
+            maximum_and_exp(EARLY, 1)
+            quantise_table(0)
+            group(0)
+            reciprocals(2)
+            quantise_table(1)
+            flip(1, 0)
+            flip(1, 1)
+
+        def step(s):
+            d = s - EARLY
+            e = s if EARLY < s < PAIRS else None
+            n = s - 1 if s <= PAIRS else None
+            g = s - 2 if s <= PAIRS + 1 else None
+            quantise(d)
+            passes(d)
+            if n is not None:
+                normalise(n)
+            if s + 2 < PAIRS:
+                last_chunk_logits(s + 2)
+            if e is not None:
+                maximum_and_exp(e, 0)
+                maximum_and_exp(e, 1)
+            if s % STEPS_A_BLOCK == 0 and s // STEPS_A_BLOCK + 1 < T // BLOCK:
+                load_x_row(s // STEPS_A_BLOCK + 1)
+            for u in range(PAIR):
+                if s + 1 < PAIRS:
+                    logits(s + 1, u)
+                if n is not None:
+                    flip(n, u)
+            if g is not None:
+                group(g)
+            drain(d)
+            if s == EARLY:
+                reciprocals(EARLY)
+            if e is not None:
+                reciprocals(e)
+
+        with tc.manual_schedule():
+            load_and_prepare()
+            start()
+            for s in range(EARLY, PAIRS + EARLY):
+                step(s)

@@ -81,6 +81,7 @@ def tile_softembedding_t_kernel(tc, input_numeric, proj_w, proj_b, emb_table, ou
         groupeds = {}
         packed = {}
         accs = {}
+        results = {}
 
         def load_and_prepare():
             nc.sync.dma_start(out=wb_raw[0:1, :], in_=proj_w.rearrange("n o -> o n"))
@@ -136,6 +137,19 @@ def tile_softembedding_t_kernel(tc, input_numeric, proj_w, proj_b, emb_table, ou
                 scales=emb_scales[:, cols],
                 in_=emb_grouped[:, cols, :].rearrange("p d j -> p (d j)"),
             )
+
+        def warm_up(count):
+            acc = ps_out.tile([P, HALF], F32, name="acc")
+            for i in range(count):
+                nc.tensor.matmul_mx(
+                    out=acc[:],
+                    lhsT=emb_codes[:, 0:P].bitcast(FP8X4),
+                    lhsT_scale=emb_scales[:, 0:P],
+                    rhs=emb_codes[:, 0:HALF].bitcast(FP8X4),
+                    rhs_scale=emb_scales[:, 0:HALF],
+                    start=True,
+                    stop=True,
+                )
 
         def last_chunk_logits(k):
             tile = logit_pool.tile([P, PAIR * P], F32, name="neg_last")
@@ -219,10 +233,15 @@ def tile_softembedding_t_kernel(tc, input_numeric, proj_w, proj_b, emb_table, ou
             )
             packed[k] = (codes, scales)
 
-        def passes(k):
+        def blocks(k, halves):
+            if k == 0:
+                return [(u, h) for h in halves for u in range(PAIR)]
+            return [(u, h) for u in range(PAIR) for h in halves]
+
+        def passes(k, halves=(0, 1)):
             codes, scales = packed[k]
-            for u in range(PAIR):
-                for h in range(D // HALF):
+            if True:
+                for u, h in blocks(k, halves):
                     acc = ps_out.tile([P, HALF], F32, name="acc")
                     nc.tensor.matmul_mx(
                         out=acc[:],
@@ -235,11 +254,13 @@ def tile_softembedding_t_kernel(tc, input_numeric, proj_w, proj_b, emb_table, ou
                     )
                     accs[(k, u, h)] = acc
 
-        def drain(k):
-            for u in range(PAIR):
-                t0 = (k * PAIR + u) * P
-                result = store.tile([P, D], F32, name="result")
-                for h in range(D // HALF):
+        def drain(k, halves=(0, 1)):
+            if True:
+                for u, h in blocks(k, halves):
+                    t0 = (k * PAIR + u) * P
+                    if h == 0:
+                        results[(k, u)] = store.tile([P, D], F32, name="result")
+                    result = results[(k, u)]
                     if (h == 0 and k >= PAIRS - TAIL) or (u, h) in VECTOR_SHARE:
                         nc.vector.tensor_copy(out=result[:, h * HALF : (h + 1) * HALF], in_=accs[(k, u, h)][:])
                     elif (u, h) == SPLIT_BANK and k < PAIRS - TAIL:
@@ -251,8 +272,8 @@ def tile_softembedding_t_kernel(tc, input_numeric, proj_w, proj_b, emb_table, ou
                     if k == PAIRS - 1:
                         cols = slice(h * HALF, (h + 1) * HALF)
                         nc.sync.dma_start(out=out_rows[t0 : t0 + P, cols], in_=result[:, cols])
-                if k < PAIRS - 1:
-                    nc.sync.dma_start(out=out_rows[t0 : t0 + P, :], in_=result[:])
+                    elif h == 1:
+                        nc.sync.dma_start(out=out_rows[t0 : t0 + P, :], in_=result[:])
 
         def start():
             logits(0, 0)
@@ -280,44 +301,51 @@ def tile_softembedding_t_kernel(tc, input_numeric, proj_w, proj_b, emb_table, ou
             flip(0, 1)
             normalise(1)
             last_chunk_logits(EARLY + 1)
+            flip(1, 0)
+            flip(1, 1)
             regroup_table("vector", 2)
             maximum_and_exp(EARLY, 0)
             maximum_and_exp(EARLY, 1)
             quantise_table(0)
+            warm_up(3)
             group(0)
+            group(1)
+            quantise(0)
             reciprocals(2)
+            passes(0, (0,))
             quantise_table(1)
-            flip(1, 0)
-            flip(1, 1)
+            drain(0, (0,))
 
         def step(s):
             d = s - EARLY
-            e = s if EARLY < s < PAIRS else None
-            n = s - 1 if s <= PAIRS else None
-            g = s - 2 if s <= PAIRS + 1 else None
-            quantise(d)
-            passes(d)
-            if n is not None:
-                normalise(n)
+            if s > EARLY:
+                quantise(d)
+                passes(d)
+            else:
+                passes(d, (1,))
+            if s <= PAIRS:
+                normalise(s - 1)
             if s + 2 < PAIRS:
                 last_chunk_logits(s + 2)
-            if e is not None:
-                maximum_and_exp(e, 0)
-                maximum_and_exp(e, 1)
+            if EARLY < s < PAIRS:
+                maximum_and_exp(s, 0)
+                maximum_and_exp(s, 1)
             if s % STEPS_A_BLOCK == 0 and s // STEPS_A_BLOCK + 1 < T // BLOCK:
                 load_x_row(s // STEPS_A_BLOCK + 1)
             for u in range(PAIR):
                 if s + 1 < PAIRS:
                     logits(s + 1, u)
-                if n is not None:
-                    flip(n, u)
-            if g is not None:
-                group(g)
-            drain(d)
+                if s <= PAIRS:
+                    flip(s - 1, u)
+            if EARLY < s <= PAIRS + 1:
+                group(s - 2)
             if s == EARLY:
-                reciprocals(EARLY)
-            if e is not None:
-                reciprocals(e)
+                reciprocals(s)
+                drain(d, (1,))
+            else:
+                drain(d)
+            if EARLY < s < PAIRS:
+                reciprocals(s)
 
         with tc.manual_schedule():
             load_and_prepare()

@@ -30,6 +30,7 @@ ROW_TILES = 2
 ONES_ROW = 1
 FIRST = 2 * PAIR * P
 TWO_ONES = 1.0019378662109375
+BY_BANK = 4
 TAIL = 2
 VECTOR_SHARE = ((0, 0),)
 
@@ -269,7 +270,7 @@ def tile_softembedding_t_kernel(tc, input_numeric, proj_w, proj_b, emb_table, ou
                         nc.scalar.copy(out=result[:, cut : (h + 1) * HALF], in_=accs[(k, u, h)][:, SLICE:HALF])
                     else:
                         nc.scalar.copy(out=result[:, h * HALF : (h + 1) * HALF], in_=accs[(k, u, h)][:])
-                    if k == PAIRS - 1:
+                    if k >= PAIRS - BY_BANK:
                         cols = slice(h * HALF, (h + 1) * HALF)
                         nc.sync.dma_start(out=out_rows[t0 : t0 + P, cols], in_=result[:, cols])
                     elif h == 1:

@@ -35,7 +35,7 @@ TAIL = 2
 VECTOR_SHARE = ((0, 0),)
 
 SPLIT_BANK = (1, 1)
-SLICE = 128
+SLICE = 112
 
 FLOPS = 2 * T * N * D
 
@@ -123,7 +123,12 @@ def tile_softembedding_t_kernel(tc, input_numeric, proj_w, proj_b, emb_table, ou
         def regroup_table(engine, quarter):
             first = quarter % 2 * QUARTER
             target = emb_grouped[:, quarter * QUARTER : (quarter + 1) * QUARTER, :]
-            source = emb_raw[quarter // 2][:, :, first : first + QUARTER].rearrange("p j d -> p d j")
+            source = emb_raw[quarter // 2][:, :, first : first + QUARTER]
+            if engine == "gpsimd":
+                source = source.rearrange("p j d -> p d j")
+            else:
+                target = target.rearrange("p (c i) j -> p c j i", i=PACK)
+                source = source.rearrange("p j (c i) -> p c j i", i=PACK)
             if engine == "gpsimd":
                 nc.gpsimd.tensor_scalar(out=target, in0=source, scalar1=1.0, scalar2=0.0, op0=ALU.mult, op1=ALU.add)
             elif engine == "scalar":

@@ -185,18 +185,25 @@ def tile_softembedding_t_kernel(tc, input_numeric, proj_w, proj_b, emb_table, ou
                 nc.tensor.transpose(bank[:, MM_CHUNKS * P : N], last_chunk[k][:, u * P : (u + 1) * P], ident_f32[:])
             banks[(k, u)] = bank
 
-        def maximum_and_exp(k, u):
+        def maximum(k, u):
             if u == 0:
                 neg_maxima[k] = small.tile([P, PAIR], F32, name="neg_max")
                 totals[k] = small.tile([P, PAIR], F32, name="total")
             bank = banks[(k, u)]
             nc.vector.tensor_reduce(out=neg_maxima[k][:, u : u + 1], in_=bank[:], axis=AX.X, op=ALU.min)
+
+        def exp(k, u):
+            bank = banks[(k, u)]
             e = work.tile([P, N], F32, name="exps")
             nc.scalar.activation(
                 out=e[:], in_=bank[:], func=ACT.Exp, bias=neg_maxima[k][:, u : u + 1], scale=-1.0,
                 accum_out=totals[k][:, u : u + 1],
             )
             exps[(k, u)] = e
+
+        def maximum_and_exp(k, u):
+            maximum(k, u)
+            exp(k, u)
 
         def reciprocals(k):
             inverse = small.tile([P, PAIR], F32, name="inverse")
@@ -288,39 +295,42 @@ def tile_softembedding_t_kernel(tc, input_numeric, proj_w, proj_b, emb_table, ou
             for k in range(1, EARLY):
                 logits(k, 0)
                 logits(k, 1)
+            regroup_table("scalar", 1)
             regroup_table("gpsimd", 0)
-            regroup_table("gpsimd", 1)
+            regroup_table("gpsimd", 3)
             maximum_and_exp(0, 0)
             maximum_and_exp(0, 1)
-            keep_last_chunk()
             maximum_and_exp(1, 0)
             maximum_and_exp(1, 1)
+            maximum(2, 0)
             reciprocals(0)
-            normalise(0, engine="scalar")
+            maximum(2, 1)
+            keep_last_chunk()
             logits(EARLY, 0)
             logits(EARLY, 1)
-            maximum_and_exp(2, 0)
-            maximum_and_exp(2, 1)
-            regroup_table("scalar", 3)
-            reciprocals(1)
+            normalise(0, (0,), engine="scalar")
+            normalise(0, (1,))
+            exp(2, 0)
+            exp(2, 1)
             flip(0, 0)
             flip(0, 1)
-            normalise(1)
-            last_chunk_logits(EARLY + 1)
-            flip(1, 0)
-            flip(1, 1)
-            regroup_table("vector", 2)
             maximum_and_exp(EARLY, 0)
-            maximum_and_exp(EARLY, 1)
             quantise_table(0)
-            warm_up(3)
+            warm_up(2)
+            regroup_table("vector", 2)
             group(0)
-            group(1)
-            quantise(0)
+            reciprocals(1)
             reciprocals(2)
+            normalise(1, engine="scalar")
+            last_chunk_logits(EARLY + 1)
+            quantise(0)
             passes(0, (0,))
             quantise_table(1)
+            maximum_and_exp(EARLY, 1)
+            flip(1, 0)
+            flip(1, 1)
             drain(0, (0,))
+            group(1)
 
         def step(s):
             d = s - EARLY

@@ -30,7 +30,7 @@ ROW_TILES = 2
 ONES_ROW = 1
 FIRST = 2 * PAIR * P
 TWO_ONES = 1.0019378662109375
-BY_BANK = 4
+BY_BANK = 1
 TAIL = 2
 VECTOR_SHARE = ((0, 0),)
 

from contextlib import ExitStack

import concourse.mybir as mybir
from concourse.masks import make_identity

F32 = mybir.dt.float32
BF16 = mybir.dt.bfloat16
U32 = mybir.dt.uint32
U8 = mybir.dt.uint8
FP8X4 = mybir.dt.float8_e4m3fn_x4
ALU = mybir.AluOpType
ACT = mybir.ActivationFunctionType
AX = mybir.AxisListType

P = 128
PACK = 4
HALVES = 2
T = 32 * 256
N = 512
D = 1024
HALF = 512
PAIR = 2
PAIRS = T // (P * PAIR)
MM_CHUNKS = 3
BLOCK = 1024
STEPS_A_BLOCK = BLOCK // (P * PAIR)
EARLY = 3
QUARTER = 256
ROW_TILES = 2
ONES_ROW = 1
FIRST = 2 * PAIR * P
TWO_ONES = 1.0019378662109375
BY_BANK = 1
TAIL = 2
VECTOR_SHARE = ((0, 0),)

SPLIT_BANK = (1, 1)
SLICE = 112

FLOPS = 2 * T * N * D


def tile_softembedding_t_kernel(tc, input_numeric, proj_w, proj_b, emb_table, out):
    nc = tc.nc
    x_row = input_numeric.rearrange("b s o -> o (b s)")
    x_flat = input_numeric.rearrange("b s o -> (b s o)")
    out_rows = out.rearrange("b s d -> (b s) d")

    with ExitStack() as ctx:
        keep = ctx.enter_context(tc.tile_pool(name="keep", bufs=1))
        logit_pool = ctx.enter_context(tc.tile_pool(name="logit", bufs=4))
        work = ctx.enter_context(tc.tile_pool(name="work", bufs=6))
        small = ctx.enter_context(tc.tile_pool(name="small", bufs=6))
        quant = ctx.enter_context(tc.tile_pool(name="quant", bufs=3))
        store = ctx.enter_context(tc.tile_pool(name="store", bufs=6))
        ps_logit = ctx.enter_context(tc.psum_pool(name="ps_logit", bufs=2))
        ps_flip = ctx.enter_context(tc.psum_pool(name="ps_flip", bufs=2))
        ps_out = ctx.enter_context(tc.psum_pool(name="ps_out", bufs=4))

        wb_raw = keep.tile([P, N], BF16)
        x_rows = [keep.tile([P, BLOCK], BF16, name="x_rows_%d" % i) for i in range(ROW_TILES)]
        x_all = keep.tile([P, T], BF16)
        emb_raw = [keep.tile([P, PACK, HALF], BF16, name="emb_raw_%d" % h) for h in range(D // HALF)]
        ident_f32 = keep.tile([P, P], F32)
        wb_neg = keep.tile([P, N], BF16)
        wb_last = keep.tile([P, P], F32)
        neg_last = keep.tile([P, 2], F32)
        warm = keep.tile([P, 1], F32)
        emb_grouped = keep.tile([P, D, PACK], BF16, align_bytes=64)
        emb_codes = keep.tile([P, D], U32, align_bytes=64)
        emb_scales = keep.tile([P, D], U8, align_bytes=64)

        corners = []
        last_chunk = {}
        banks = {}
        exps = {}
        totals = {}
        neg_maxima = {}
        inverses = {}
        weights = {}
        flips = {}
        groupeds = {}
        packed = {}
        accs = {}
        results = {}

        def load_and_prepare():
            nc.sync.dma_start(out=wb_raw[0:1, :], in_=proj_w.rearrange("n o -> o n"))
            nc.sync.dma_start(out=wb_raw[ONES_ROW : ONES_ROW + 1, :], in_=proj_b.rearrange("(o n) -> o n", o=1))
            nc.gpsimd.memset(x_rows[0][:, 0:FIRST].bitcast(F32), TWO_ONES)
            nc.sync.dma_start(out=x_rows[0][0:1, 0:FIRST], in_=x_row[:, 0:FIRST])
            for h in range(D // HALF):
                cols = slice(h * HALF, (h + 1) * HALF)
                nc.sync.dma_start(out=emb_raw[h][:], in_=emb_table[:, cols].rearrange("(p j) d -> p j d", j=PACK))
            nc.gpsimd.memset(wb_neg[:].bitcast(F32), 0.0)
            nc.gpsimd.memset(x_rows[0][:, FIRST:BLOCK].bitcast(F32), TWO_ONES)
            nc.sync.dma_start(out=x_rows[0][0:1, FIRST:BLOCK], in_=x_row[:, FIRST:BLOCK])
            nc.gpsimd.memset(x_rows[1][:].bitcast(F32), TWO_ONES)
            make_identity(nc, ident_f32[:])
            nc.scalar.activation(out=warm[:], in_=x_rows[1][:, 0:2].bitcast(F32), func=ACT.Exp)
            for t0, t1 in ((BLOCK, 2 * BLOCK), (2 * BLOCK, T)):
                nc.sync.dma_start(out=x_all[:, t0:t1], in_=x_flat[t0:t1].partition_broadcast(P))
            load_x_row(1)
            nc.vector.tensor_scalar(
                out=wb_neg[0 : ONES_ROW + 1, :].rearrange("p (h i e) -> p h i e", h=HALVES, e=2),
                in0=wb_raw[0 : ONES_ROW + 1, :].rearrange("p (i h e) -> p h i e", h=HALVES, e=2),
                scalar1=-1.0, scalar2=None, op0=ALU.mult,
            )
            nc.vector.tensor_copy(out=wb_last[:], in_=wb_neg[:, MM_CHUNKS * P : N])

        def load_x_row(block):
            t0 = block * BLOCK
            nc.sync.dma_start(out=x_rows[block % ROW_TILES][0:1, :], in_=x_row[:, t0 : t0 + BLOCK])

        def flip_last_chunk():
            corner = ps_flip.tile([P, P], F32, name="flipped")
            nc.tensor.transpose(corner[:], wb_last[:], ident_f32[:])
            corners.append(corner)

        def keep_last_chunk():
            nc.vector.tensor_copy(out=neg_last[:], in_=corners[0][:, 0 : 2 * ONES_ROW : ONES_ROW])

        def regroup_table(engine, quarter):
            first = quarter % 2 * QUARTER
            target = emb_grouped[:, quarter * QUARTER : (quarter + 1) * QUARTER, :]
            source = emb_raw[quarter // 2][:, :, first : first + QUARTER]
            if engine == "gpsimd":
                source = source.rearrange("p j d -> p d j")
            else:
                target = target.rearrange("p (c i) j -> p c j i", i=PACK)
                source = source.rearrange("p j (c i) -> p c j i", i=PACK)
            if engine == "gpsimd":
                nc.gpsimd.tensor_scalar(out=target, in0=source, scalar1=1.0, scalar2=0.0, op0=ALU.mult, op1=ALU.add)
            elif engine == "scalar":
                nc.scalar.copy(out=target, in_=source)
            else:
                nc.vector.tensor_copy(out=target, in_=source)

        def quantise_table(half):
            cols = slice(half * HALF, (half + 1) * HALF)
            nc.vector.quantize_mx(
                out=emb_codes[:, cols].bitcast(FP8X4),
                scales=emb_scales[:, cols],
                in_=emb_grouped[:, cols, :].rearrange("p d j -> p (d j)"),
            )

        def warm_up(count):
            acc = ps_out.tile([P, HALF], F32, name="acc")
            for i in range(count):
                nc.tensor.matmul_mx(
                    out=acc[:],
                    lhsT=emb_codes[:, 0:P].bitcast(FP8X4),
                    lhsT_scale=emb_scales[:, 0:P],
                    rhs=emb_codes[:, 0:HALF].bitcast(FP8X4),
                    rhs_scale=emb_scales[:, 0:HALF],
                    start=True,
                    stop=True,
                )

        def last_chunk_logits(k):
            tile = logit_pool.tile([P, PAIR * P], F32, name="neg_last")
            nc.gpsimd.tensor_scalar(
                out=tile[:],
                in0=x_all[:, k * PAIR * P : (k + 1) * PAIR * P],
                scalar1=neg_last[:, 0:1],
                scalar2=neg_last[:, 1:2],
                op0=ALU.mult,
                op1=ALU.add,
            )
            last_chunk[k] = tile

        def logits(k, u):
            spare = 0 < k < EARLY
            t0 = (k * PAIR + u) * P
            chunks = PACK if t0 < BLOCK else MM_CHUNKS
            bank = ps_out.tile([P, N], F32, name="acc") if spare else ps_logit.tile([P, N], F32, name="bank")
            nc.tensor.matmul(
                out=bank[:, 0 : chunks * P],
                lhsT=x_rows[t0 // BLOCK % ROW_TILES][:, t0 % BLOCK : t0 % BLOCK + P],
                rhs=wb_neg[:, 0 : chunks * P],
                start=True,
                stop=True,
            )
            if chunks < PACK:
                nc.tensor.transpose(bank[:, MM_CHUNKS * P : N], last_chunk[k][:, u * P : (u + 1) * P], ident_f32[:])
            banks[(k, u)] = bank

        def maximum(k, u):
            if u == 0:
                neg_maxima[k] = small.tile([P, PAIR], F32, name="neg_max")
                totals[k] = small.tile([P, PAIR], F32, name="total")
            bank = banks[(k, u)]
            nc.vector.tensor_reduce(out=neg_maxima[k][:, u : u + 1], in_=bank[:], axis=AX.X, op=ALU.min)

        def exp(k, u):
            bank = banks[(k, u)]
            e = work.tile([P, N], F32, name="exps")
            nc.scalar.activation(
                out=e[:], in_=bank[:], func=ACT.Exp, bias=neg_maxima[k][:, u : u + 1], scale=-1.0,
                accum_out=totals[k][:, u : u + 1],
            )
            exps[(k, u)] = e

        def maximum_and_exp(k, u):
            maximum(k, u)
            exp(k, u)

        def reciprocals(k):
            inverse = small.tile([P, PAIR], F32, name="inverse")
            nc.vector.reciprocal(out=inverse[:], in_=totals[k][:])
            inverses[k] = inverse

        def normalise(k, tiles=(0, 1), engine="gpsimd"):
            for u in tiles:
                w = work.tile([P, N], BF16, name="weights")
                if engine == "scalar":
                    nc.scalar.activation(out=w[:], in_=exps[(k, u)][:], func=ACT.Copy, scale=inverses[k][:, u : u + 1])
                elif k == PAIRS - 1:
                    nc.vector.tensor_scalar(
                        out=w[:], in0=exps[(k, u)][:], scalar1=inverses[k][:, u : u + 1], scalar2=None, op0=ALU.mult
                    )
                else:
                    nc.gpsimd.tensor_scalar(
                        out=w[:], in0=exps[(k, u)][:], scalar1=inverses[k][:, u : u + 1], scalar2=0.0,
                        op0=ALU.mult, op1=ALU.add,
                    )
                weights[(k, u)] = w

        def flip(k, u):
            if u == 0:
                flips[k] = ps_flip.tile([P, PAIR, HALVES, P], F32, name="flipped")
            words = weights[(k, u)][:].bitcast(F32)
            for h in range(HALVES):
                nc.tensor.transpose(flips[k][:, u, h, :], words[:, h * P : (h + 1) * P], ident_f32[:])

        def group(k):
            grouped = quant.tile([P, PAIR, P, PACK], BF16, name="grouped", align_bytes=64)
            nc.vector.tensor_copy(out=grouped[:].bitcast(F32), in_=flips[k][:].rearrange("p u h t -> p u t h"))
            groupeds[k] = grouped

        def quantise(k):
            codes = quant.tile([P, PAIR * P], U32, name="codes", align_bytes=64)
            scales = quant.tile([P, PAIR * P], U8, name="scales", align_bytes=64)
            nc.vector.quantize_mx(
                out=codes[:].bitcast(FP8X4), scales=scales[:], in_=groupeds[k][:].rearrange("p u t c -> p (u t c)")
            )
            packed[k] = (codes, scales)

        def blocks(k, halves):
            if k == 0:
                return [(u, h) for h in halves for u in range(PAIR)]
            return [(u, h) for u in range(PAIR) for h in halves]

        def passes(k, halves=(0, 1)):
            codes, scales = packed[k]
            if True:
                for u, h in blocks(k, halves):
                    acc = ps_out.tile([P, HALF], F32, name="acc")
                    nc.tensor.matmul_mx(
                        out=acc[:],
                        lhsT=codes[:, u * P : (u + 1) * P].bitcast(FP8X4),
                        lhsT_scale=scales[:, u * P : (u + 1) * P],
                        rhs=emb_codes[:, h * HALF : (h + 1) * HALF].bitcast(FP8X4),
                        rhs_scale=emb_scales[:, h * HALF : (h + 1) * HALF],
                        start=True,
                        stop=True,
                    )
                    accs[(k, u, h)] = acc

        def drain(k, halves=(0, 1)):
            if True:
                for u, h in blocks(k, halves):
                    t0 = (k * PAIR + u) * P
                    if h == 0:
                        results[(k, u)] = store.tile([P, D], F32, name="result")
                    result = results[(k, u)]
                    if (h == 0 and k >= PAIRS - TAIL) or (u, h) in VECTOR_SHARE:
                        nc.vector.tensor_copy(out=result[:, h * HALF : (h + 1) * HALF], in_=accs[(k, u, h)][:])
                    elif (u, h) == SPLIT_BANK and k < PAIRS - TAIL:
                        cut = h * HALF + SLICE
                        nc.vector.tensor_copy(out=result[:, h * HALF : cut], in_=accs[(k, u, h)][:, 0:SLICE])
                        nc.scalar.copy(out=result[:, cut : (h + 1) * HALF], in_=accs[(k, u, h)][:, SLICE:HALF])
                    else:
                        nc.scalar.copy(out=result[:, h * HALF : (h + 1) * HALF], in_=accs[(k, u, h)][:])
                    if k >= PAIRS - BY_BANK:
                        cols = slice(h * HALF, (h + 1) * HALF)
                        nc.sync.dma_start(out=out_rows[t0 : t0 + P, cols], in_=result[:, cols])
                    elif h == 1:
                        nc.sync.dma_start(out=out_rows[t0 : t0 + P, :], in_=result[:])

        def start():
            logits(0, 0)
            logits(0, 1)
            flip_last_chunk()
            for k in range(1, EARLY):
                logits(k, 0)
                logits(k, 1)
            regroup_table("scalar", 1)
            regroup_table("gpsimd", 0)
            regroup_table("gpsimd", 3)
            maximum_and_exp(0, 0)
            maximum_and_exp(0, 1)
            maximum_and_exp(1, 0)
            maximum_and_exp(1, 1)
            maximum(2, 0)
            reciprocals(0)
            maximum(2, 1)
            keep_last_chunk()
            logits(EARLY, 0)
            logits(EARLY, 1)
            normalise(0, (0,), engine="scalar")
            normalise(0, (1,))
            exp(2, 0)
            exp(2, 1)
            flip(0, 0)
            flip(0, 1)
            maximum_and_exp(EARLY, 0)
            quantise_table(0)
            warm_up(2)
            regroup_table("vector", 2)
            group(0)
            reciprocals(1)
            reciprocals(2)
            normalise(1, engine="scalar")
            last_chunk_logits(EARLY + 1)
            quantise(0)
            passes(0, (0,))
            quantise_table(1)
            maximum_and_exp(EARLY, 1)
            flip(1, 0)
            flip(1, 1)
            drain(0, (0,))
            group(1)

        def step(s):
            d = s - EARLY
            if s > EARLY:
                quantise(d)
                passes(d)
            else:
                passes(d, (1,))
            if s <= PAIRS:
                normalise(s - 1)
            if s + 2 < PAIRS:
                last_chunk_logits(s + 2)
            if EARLY < s < PAIRS:
                maximum_and_exp(s, 0)
                maximum_and_exp(s, 1)
            if s % STEPS_A_BLOCK == 0 and s // STEPS_A_BLOCK + 1 < T // BLOCK:
                load_x_row(s // STEPS_A_BLOCK + 1)
            for u in range(PAIR):
                if s + 1 < PAIRS:
                    logits(s + 1, u)
                if s <= PAIRS:
                    flip(s - 1, u)
            if EARLY < s <= PAIRS + 1:
                group(s - 2)
            if s == EARLY:
                reciprocals(s)
                drain(d, (1,))
            else:
                drain(d)
            if EARLY < s < PAIRS:
                reciprocals(s)

        with tc.manual_schedule():
            load_and_prepare()
            start()
            for s in range(EARLY, PAIRS + EARLY):
                step(s)
